import numpy as np
import ml_dtypes


def mxq(x, axis, fmt="e4m3"):
    dtype, down = {"e4m3": (ml_dtypes.float8_e4m3fn, 7), "e5m2": (ml_dtypes.float8_e5m2, 14)}[fmt]
    v = np.moveaxis(np.asarray(x, np.float32).astype(ml_dtypes.bfloat16).astype(np.float64), axis, -1)
    blocks = v.reshape(v.shape[:-1] + (-1, 32))
    amax = np.abs(blocks).max(-1, keepdims=True)
    byte = np.maximum(np.where(amax > 0, np.frexp(amax)[1] - 1 + 127, 0) - down, 1)
    scale = np.exp2(byte - 127.0)
    codes = (blocks / scale).astype(np.float32).astype(dtype).astype(np.float64)
    return np.moveaxis((codes * scale).reshape(v.shape), -1, axis)


WIDE = False


def mx_kscale(k):
    if not WIDE:
        return np.ones(k)
    levels = np.array([10, -10, 5, -5, 0])
    a = np.random.permutation(np.resize(levels, k // 512 * 4)).reshape(k // 512, 4)
    idx = np.arange(k)
    return np.exp2(a[idx // 512, idx % 128 // 32])


BF16 = ml_dtypes.bfloat16


def bf(x):
    return np.asarray(x, np.float32).astype(BF16)


def f64(x):
    return np.asarray(x).astype(np.float64)


B, L, V, N = 2, 2048, 1024, 512


def _sanitize(x):
    return np.nan_to_num(x, nan=0.0, posinf=1e4, neginf=-1e4)


def _safe_acosh(x):
    xm1 = np.maximum(x - 1.0, 0.0)
    near = xm1 < 1e-3
    taylor = np.sqrt(2.0 * np.maximum(xm1, 1e-12)) * (1.0 - xm1 / 12.0)
    exact = np.arccosh(np.maximum(x, 1.0 + 1e-7))
    return np.where(near, taylor, exact)


def setup_inputs():
    s = mx_kscale(N)
    c = np.exp2(np.round(0.5 * np.log2(np.mean(1.0 / (s * s)))))
    m = np.random.standard_normal(N)
    sp = (np.random.standard_normal((B, L, N)) + np.random.uniform(-1.5, 1.5, (B, L, 1)) * m) / np.sqrt(N)
    t = np.sqrt(1.0 + np.sum(sp * sp, axis=-1, keepdims=True))
    w = (np.random.standard_normal((V, N)) + np.random.uniform(-1.5, 1.5, (V, 1)) * m) * 0.7 / np.sqrt(N)
    return {"hidden_states": bf(np.concatenate([t, sp * (s * c)], axis=-1)), "weight": bf(w / (s * c)),
            "logit_scale": bf(0.6 + 0.1 * np.random.standard_normal(1))}


def reference(hidden_states, weight, logit_scale):
    h = _sanitize(f64(hidden_states))
    weight = f64(weight)
    norm = np.linalg.norm(weight, axis=-1)
    r = np.where(norm > 1e-7, np.sinh(norm) / np.maximum(norm, 1e-7), 1.0)
    w_time = np.cosh(norm)
    w_space = r[:, None] * weight
    dot = mxq(h[..., 1:], 2, "e4m3") @ mxq(w_space, 1, "e4m3").T
    x = h[..., :1] * w_time[None, None, :] - dot
    d = _safe_acosh(x)
    tau = np.clip(f64(logit_scale), 0.01, 2.5)
    logits = -tau * d * d
    return _sanitize(logits)

@@ -1,0 +1,491 @@
+from contextlib import ExitStack
+
+import concourse.mybir as mybir
+from concourse.masks import make_identity
+
+F32 = mybir.dt.float32
+BF16 = mybir.dt.bfloat16
+U32 = mybir.dt.uint32
+U8 = mybir.dt.uint8
+FP8X4 = mybir.dt.float8_e4m3fn_x4
+ALU = mybir.AluOpType
+ACT = mybir.ActivationFunctionType
+
+P = 128
+TOKENS = 4096
+VOCAB = 1024
+K = 512
+BANK = 512
+TILES = TOKENS // P
+CHUNK = 8
+GROUP = 4
+GROUPS = TILES // GROUP
+W_TILES = VOCAB // P
+SLOT = 528
+FMAX = 3.3895313892515355e38
+C_INF = 1.0e4 / FMAX
+SUMSQ_MAX = 7.0e3
+FLOPS = 2 * TOKENS * VOCAB * K
+
+BATCHES = (10, 10)
+LOOKAHEAD = 4
+X_TILES = 5
+A_TILES = 9
+SANITISE_LEAD = 4
+TRANSPOSE_LAG = 2
+QUANTISE_LAG = 1
+SCALAR_CLIPS = 7
+FIRST_PULLS = 3
+
+
+def make_units():
+    units = [[(0, 0)], [(1, 0)], [(2, 0), (3, 0)], [(i, 1) for i in range(GROUP)]]
+    place = [(0, 0), (0, 1), (0, 2), (1, 0)]
+    for i in range(GROUP, TILES - 2, 2):
+        place.append((len(units) - 2, 0))
+        units.append([(i, 0), (i, 1), (i + 1, 0), (i + 1, 1)])
+    last = len(units) - 2
+    units.extend([[(TILES - 2, 0), (TILES - 2, 1)], [(TILES - 1, 0)], [(TILES - 1, 1)]])
+    place.extend([(last, 0), (last, 2), (last, 3)])
+    return units, place
+
+
+def tile_geodesiclmheadv2_t_kernel(tc, hidden_states, weight, logit_scale, out):
+    nc = tc.nc
+    hid = hidden_states.flatten_outer_dims().rearrange("(p i) c -> p i c", i=TILES)
+    out_tiles = out.flatten_outer_dims().rearrange("(p i) v -> p i v", i=TILES)
+    out_flat = out.flatten_outer_dims().rearrange("(p i) v -> p (i v)", i=TILES)
+    w_rows = weight.rearrange("(j p) k -> p j k", p=P)
+    units, place = make_units()
+    n_units = len(units)
+
+    with ExitStack() as ctx:
+        keep = ctx.enter_context(tc.tile_pool(name="keep", bufs=1))
+        grouped_pool = ctx.enter_context(tc.tile_pool(name="grouped", bufs=3))
+        x_pool = ctx.enter_context(tc.tile_pool(name="x", bufs=X_TILES))
+        a_pool = ctx.enter_context(tc.tile_pool(name="a", bufs=A_TILES))
+        turn_pool = ctx.enter_context(tc.psum_pool(name="turn", bufs=4))
+        sum_pool = ctx.enter_context(tc.psum_pool(name="sum", bufs=4))
+        ctx.enter_context(tc.manual_schedule())
+
+        ident = keep.tile([P, P], F32, name="ident")
+        one = keep.tile([P, 1], F32, name="one")
+        minus_one = keep.tile([P, 1], F32, name="minus_one")
+        floor_b = keep.tile([P, 1], F32, name="floor_b")
+        scratch = keep.tile([P, 1], F32, name="scratch")
+        ident_bf = keep.tile([P, P], BF16, name="ident_bf")
+        make_identity(nc, ident[:])
+        make_identity(nc, ident_bf[:])
+        nc.vector.memset(one[:], 1.0)
+        nc.vector.memset(minus_one[:], -1.0)
+        nc.vector.memset(floor_b[:], 0.5e-12)
+        nc.scalar.activation(out=scratch[:], in_=one[:], func=ACT.Sqrt)
+
+        w_raw = [keep.tile([P, 2 * K], BF16, name="w_raw%d" % q) for q in range(W_TILES // 2)]
+        for q in range(W_TILES // 2):
+            nc.sync.dma_start(
+                out=w_raw[q][:].rearrange("p (j k) -> p j k", k=K), in_=w_rows[:, 2 * q : 2 * q + 2, :]
+            )
+        h_raw = [keep.tile([P, CHUNK * SLOT], BF16, name="h_raw%d" % c) for c in range(TILES // CHUNK)]
+        scale_raw = keep.tile([P, 1], BF16, name="scale_raw")
+        for c in range(TILES // CHUNK):
+            nc.sync.dma_start(
+                out=h_raw[c][:].rearrange("p (i c) -> p i c", c=SLOT)[:, :, 1 : K + 2],
+                in_=hid[:, CHUNK * c : CHUNK * (c + 1), :],
+            )
+            if c == 0:
+                nc.sync.dma_start(out=scale_raw[:], in_=logit_scale.partition_broadcast(P))
+
+        def nan_to_num_factor(eng, up, down, x):
+            eng.tensor_scalar(out=up, in0=x, scalar1=FMAX, scalar2=C_INF, op0=ALU.is_le, op1=ALU.add)
+            eng.tensor_scalar(out=down, in0=x, scalar1=-FMAX, scalar2=C_INF, op0=ALU.is_ge, op1=ALU.add)
+
+        t_raw = keep.tile([P, TILES], F32, name="t_raw")
+        t_up = keep.tile([P, TILES], F32, name="t_up")
+        t_down = keep.tile([P, TILES], F32, name="t_down")
+        t_coord = keep.tile([P, TILES], F32, name="t_coord")
+
+        def time_coordinates(c0, c1):
+            for c in range(c0, c1):
+                nc.gpsimd.tensor_copy(
+                    out=t_raw[:, CHUNK * c : CHUNK * (c + 1)].unsqueeze(2),
+                    in_=h_raw[c][:].rearrange("p (i c) -> p i c", c=SLOT)[:, :, 1:2],
+                )
+            s = slice(CHUNK * c0, CHUNK * c1)
+            nan_to_num_factor(nc.gpsimd, t_up[:, s], t_down[:, s], t_raw[:, s])
+            nc.gpsimd.tensor_tensor(out=t_up[:, s], in0=t_up[:, s], in1=t_down[:, s], op=ALU.mult)
+            nc.gpsimd.tensor_scalar(
+                out=t_raw[:, s], in0=t_raw[:, s], scalar1=-FMAX, scalar2=FMAX, op0=ALU.max, op1=ALU.min
+            )
+            nc.gpsimd.tensor_tensor(out=t_coord[:, s], in0=t_raw[:, s], in1=t_up[:, s], op=ALU.mult)
+
+        time_coordinates(0, 1)
+        tau = keep.tile([P, 1], F32, name="tau")
+        not_neg = keep.tile([P, 1], F32, name="not_neg")
+        neg = keep.tile([P, 1], F32, name="neg")
+        minus_4tau = keep.tile([P, 1], F32, name="minus_4tau")
+        nc.gpsimd.tensor_scalar(out=tau[:], in0=scale_raw[:], scalar1=0.01, scalar2=2.5, op0=ALU.max, op1=ALU.min)
+        nc.gpsimd.tensor_scalar(out=not_neg[:], in0=scale_raw[:], scalar1=0.0, scalar2=-4.0, op0=ALU.is_ge, op1=ALU.mult)
+        nc.gpsimd.tensor_scalar(out=neg[:], in0=scale_raw[:], scalar1=0.0, scalar2=-4.0, op0=ALU.is_lt, op1=ALU.mult)
+        nc.gpsimd.tensor_tensor(out=not_neg[:], in0=not_neg[:], in1=neg[:], op=ALU.add)
+        nc.gpsimd.tensor_tensor(out=minus_4tau[:], in0=tau[:], in1=not_neg[:], op=ALU.mult)
+
+        h_codes = [keep.tile([P, GROUP * P], U32, name="h_codes%d" % g, align_bytes=64) for g in range(GROUPS)]
+        h_scales = [keep.tile([P, GROUP * P], U8, name="h_scales%d" % g, align_bytes=64) for g in range(GROUPS)]
+        factor_up = keep.tile([P, CHUNK * K], BF16, name="factor_up")
+        factor_down = keep.tile([P, CHUNK * K], BF16, name="factor_down")
+        grouped_of = {}
+        turned_of = {}
+
+        def sanitise_factor(g0, g1):
+            n = (g1 - g0) * GROUP
+            first = (g0 % 2) * GROUP
+            x = h_raw[g0 // 2][:].rearrange("p (i c) -> p i c", c=SLOT)[:, first : first + n, 2 : K + 2]
+            up = factor_up[:, 0 : n * K].rearrange("p (i c) -> p i c", c=K)
+            down = factor_down[:, 0 : n * K].rearrange("p (i c) -> p i c", c=K)
+            nan_to_num_factor(nc.vector, up, down, x)
+
+        def sanitise_apply(g0, g1):
+            n = (g1 - g0) * GROUP
+            first = (g0 % 2) * GROUP
+            x = h_raw[g0 // 2][:].rearrange("p (i c) -> p i c", c=SLOT)[:, first : first + n, 2 : K + 2]
+            nc.vector.tensor_tensor(
+                out=factor_up[:, 0 : n * K], in0=factor_up[:, 0 : n * K], in1=factor_down[:, 0 : n * K], op=ALU.mult
+            )
+            nc.vector.tensor_scalar(out=x, in0=x, scalar1=-FMAX, scalar2=FMAX, op0=ALU.max, op1=ALU.min)
+            nc.vector.tensor_tensor(
+                out=x, in0=x, in1=factor_up[:, 0 : n * K].rearrange("p (i c) -> p i c", c=K), op=ALU.mult
+            )
+
+        def h_transpose(g):
+            for pair in range(2):
+                turned = turn_pool.tile([P, BANK], F32, name="turned", tag="turn")
+                turned_of[(g, pair)] = turned
+                for ii in range(2):
+                    i = GROUP * g + 2 * pair + ii
+                    words = h_raw[i // CHUNK][:].bitcast(F32)
+                    base = (i % CHUNK) * (SLOT // 2) + 1
+                    for u in range(2):
+                        nc.tensor.transpose(
+                            out=turned[:, u * 2 * P + ii * P : u * 2 * P + (ii + 1) * P],
+                            in_=words[:, base + u * P : base + (u + 1) * P],
+                            identity=ident[:],
+                        )
+
+        def h_copy_out(g):
+            grouped_of[g] = grouped_pool.tile([P, GROUP * K], BF16, name="grouped", tag="grouped", align_bytes=64)
+            words = grouped_of[g][:].bitcast(F32).rearrange("p (t u) -> p t u", u=2)
+            for pair in range(2):
+                nc.scalar.copy(
+                    out=words[:, pair * 2 * P : (pair + 1) * 2 * P, :],
+                    in_=turned_of[(g, pair)][:].rearrange("p (u t) -> p t u", u=2),
+                )
+
+        def h_quantise(g):
+            nc.vector.quantize_mx(out=h_codes[g][:].bitcast(FP8X4), scales=h_scales[g][:], in_=grouped_of[g][:])
+
+        sumsq_s = keep.tile([P, W_TILES], F32, name="sumsq_s")
+        sumsq = keep.tile([P, W_TILES], F32, name="sumsq")
+        squares_s = keep.tile([P, K], BF16, name="squares_s")
+        squares_v = keep.tile([P, K], F32, name="squares_v")
+
+        def w_row_tile(j):
+            return w_raw[j // 2][:, (j % 2) * K : (j % 2 + 1) * K]
+
+        for j in (0, 1, 4, 5):
+            nc.scalar.activation(out=squares_s[:], in_=w_row_tile(j), func=ACT.Square, accum_out=sumsq_s[:, j : j + 1])
+        for j in (2, 3, 6, 7):
+            nc.vector.scalar_tensor_tensor(
+                out=squares_v[:], in0=w_row_tile(j), scalar=1.0, in1=w_row_tile(j), op0=ALU.mult, op1=ALU.mult,
+                accum_out=sumsq[:, j : j + 1],
+            )
+        nc.vector.tensor_copy(
+            out=sumsq[:].rearrange("p (a b) -> p a b", b=4)[:, :, 0:2],
+            in_=sumsq_s[:].rearrange("p (a b) -> p a b", b=4)[:, :, 0:2],
+        )
+        row_ok = keep.tile([P, W_TILES], F32, name="row_ok")
+        nc.vector.tensor_single_scalar(out=row_ok[:], in_=sumsq[:], scalar=FMAX, op=ALU.is_le)
+        nc.vector.tensor_scalar(out=sumsq[:], in0=sumsq[:], scalar1=1.0e-30, scalar2=SUMSQ_MAX, op0=ALU.max, op1=ALU.min)
+
+        norm = keep.tile([P, W_TILES], F32, name="norm")
+        e_plus = keep.tile([P, W_TILES], F32, name="e_plus")
+        e_minus = keep.tile([P, W_TILES], F32, name="e_minus")
+        nc.scalar.activation(out=norm[:], in_=sumsq[:], func=ACT.Sqrt)
+        nc.scalar.activation(out=e_plus[:], in_=norm[:], func=ACT.Exp)
+        nc.scalar.activation(out=e_minus[:], in_=norm[:], func=ACT.Exp, scale=-1.0)
+        nc.scalar.activation(out=scratch[:], in_=one[:], func=ACT.Sqrt)
+
+        floor_n = keep.tile([P, W_TILES], F32, name="floor_n")
+        slope = keep.tile([P, W_TILES], F32, name="slope")
+        offset = keep.tile([P, W_TILES], F32, name="offset")
+        large = keep.tile([P, W_TILES], F32, name="large")
+        diff = keep.tile([P, W_TILES], F32, name="diff")
+        total = keep.tile([P, W_TILES], F32, name="total")
+        r_col = keep.tile([P, W_TILES], F32, name="r_col")
+        cosh_col = keep.tile([P, W_TILES], F32, name="cosh_col")
+        nc.vector.tensor_scalar_max(out=floor_n[:], in0=norm[:], scalar1=1.0e-7)
+        nc.vector.reciprocal(out=slope[:], in_=floor_n[:])
+        nc.vector.tensor_single_scalar(out=large[:], in_=norm[:], scalar=1.0e-7, op=ALU.is_gt)
+        nc.vector.scalar_tensor_tensor(out=slope[:], in0=slope[:], scalar=0.5, in1=large[:], op0=ALU.mult, op1=ALU.mult)
+        nc.vector.tensor_tensor(out=slope[:], in0=slope[:], in1=row_ok[:], op=ALU.mult)
+        nc.vector.scalar_tensor_tensor(out=offset[:], in0=large[:], scalar=-1.0, in1=row_ok[:], op0=ALU.mult, op1=ALU.add)
+        nc.vector.tensor_scalar_max(out=offset[:], in0=offset[:], scalar1=0.0)
+        for q in range(W_TILES // 2):
+            nc.vector.tensor_scalar(out=w_raw[q][:], in0=w_raw[q][:], scalar1=-FMAX, scalar2=FMAX, op0=ALU.max, op1=ALU.min)
+
+        sanitise_factor(0, 1)
+        nc.vector.tensor_tensor(out=diff[:], in0=e_plus[:], in1=e_minus[:], op=ALU.subtract)
+        nc.vector.tensor_tensor(out=diff[:], in0=diff[:], in1=slope[:], op=ALU.mult)
+        nc.vector.tensor_tensor(out=r_col[:], in0=diff[:], in1=offset[:], op=ALU.add)
+        sanitise_apply(0, 1)
+        nc.vector.tensor_tensor(out=total[:], in0=e_plus[:], in1=e_minus[:], op=ALU.add)
+        nc.vector.scalar_tensor_tensor(out=cosh_col[:], in0=total[:], scalar=0.5, in1=row_ok[:], op0=ALU.mult, op1=ALU.mult)
+
+        cosh_row = keep.tile([P, VOCAB], F32, name="cosh_row")
+        spread_of = {}
+
+        def spread(column, key):
+            h = key[1]
+            bank = sum_pool.tile([P, BANK], F32, name="spread", tag="sum")
+            spread_of[key] = bank
+            for jj in range(4):
+                j = 4 * h + jj
+                nc.tensor.matmul(
+                    out=bank[:, jj * P : (jj + 1) * P],
+                    lhsT=column[:, j : j + 1].to_broadcast([P, P]),
+                    rhs=ident[:],
+                    start=True,
+                    stop=True,
+                )
+
+        def spread_copy(row, key):
+            h = key[1]
+            nc.scalar.copy(out=row[:, h * BANK : (h + 1) * BANK], in_=spread_of[key][:])
+
+        w_space = keep.tile([P, W_TILES * K], BF16, name="w_space")
+        w_grouped = [keep.tile([P, 4 * BANK], BF16, name="w_grouped%d" % h, align_bytes=64) for h in range(2)]
+        w_codes = keep.tile([P, VOCAB], U32, name="w_codes", align_bytes=64)
+        w_scales = keep.tile([P, VOCAB], U8, name="w_scales", align_bytes=64)
+        w_turned = {}
+
+        def w_scale(j):
+            nc.scalar.activation(
+                out=w_space[:, j * K : (j + 1) * K].rearrange("p (u e q) -> p u e q", u=2, e=2),
+                in_=w_row_tile(j).rearrange("p (u q e) -> p u e q", u=2, e=2),
+                func=ACT.Copy,
+                scale=r_col[:, j : j + 1],
+            )
+
+        def w_transpose(q):
+            turned = turn_pool.tile([P, 2 * BANK], BF16, name="w_turned", tag="turn")
+            w_turned[q] = turned
+            for jj in range(2):
+                for t in range(4):
+                    nc.tensor.transpose(
+                        out=turned[:, (jj * 4 + t) * P : (jj * 4 + t + 1) * P],
+                        in_=w_space[:, (2 * q + jj) * K + t * P : (2 * q + jj) * K + (t + 1) * P],
+                        identity=ident_bf[:],
+                    )
+
+        def w_copy_out(q):
+            nc.scalar.copy(
+                out=w_grouped[q // 2][:, (q % 2) * 2 * BANK : (q % 2 + 1) * 2 * BANK].rearrange(
+                    "p (j v t) -> p j v t", j=2, t=4
+                ),
+                in_=w_turned[q][:].rearrange("p (j t v) -> p j v t", j=2, t=4),
+            )
+
+        def w_quantise(h):
+            nc.vector.quantize_mx(
+                out=w_codes[:, h * BANK : (h + 1) * BANK].bitcast(FP8X4),
+                scales=w_scales[:, h * BANK : (h + 1) * BANK],
+                in_=w_grouped[h][:],
+            )
+
+        def w_side(h):
+            for j in range(4 * h, 4 * h + 4):
+                w_scale(j)
+            w_transpose(2 * h)
+            w_transpose(2 * h + 1)
+            if h == 0:
+                h_transpose(0)
+            spread(cosh_col, ("cosh", h))
+            w_copy_out(2 * h)
+            w_copy_out(2 * h + 1)
+            if h == 0:
+                h_copy_out(0)
+            spread_copy(cosh_row, ("cosh", h))
+            w_quantise(h)
+
+        w_side(0)
+        h_quantise(0)
+
+        dot_of = {}
+        x_of = {}
+        a_of = {}
+
+        def columns(u):
+            first = place[u][1] * BANK
+            return slice(first, first + len(units[u]) * BANK)
+
+        def dot(u):
+            for k, (i, h) in enumerate(units[u]):
+                g = i // GROUP
+                tokens = slice((i % GROUP) * P, (i % GROUP + 1) * P)
+                bank = sum_pool.tile([P, BANK], F32, name="dot", tag="sum")
+                dot_of[(u, k)] = bank
+                nc.tensor.matmul_mx(
+                    out=bank[:],
+                    lhsT=h_codes[g][:, tokens].bitcast(FP8X4),
+                    lhsT_scale=h_scales[g][:, tokens],
+                    rhs=w_codes[:, h * BANK : (h + 1) * BANK].bitcast(FP8X4),
+                    rhs_scale=w_scales[:, h * BANK : (h + 1) * BANK],
+                    start=True,
+                    stop=True,
+                )
+
+        def make_x(u):
+            tile_no, first = place[u]
+            if tile_no not in x_of:
+                x_of[tile_no] = x_pool.tile([P, 4 * BANK], F32, name="x", tag="x")
+            x = x_of[tile_no]
+            for k, (i, h) in enumerate(units[u]):
+                nc.vector.scalar_tensor_tensor(
+                    out=x[:, (first + k) * BANK : (first + k + 1) * BANK],
+                    in0=cosh_row[:, h * BANK : (h + 1) * BANK],
+                    scalar=t_coord[:, i : i + 1],
+                    in1=dot_of[(u, k)][:],
+                    op0=ALU.mult,
+                    op1=ALU.subtract,
+                )
+            if u >= SCALAR_CLIPS:
+                c = columns(u)
+                nc.vector.tensor_scalar(out=x[:, c], in0=x[:, c], scalar1=-1.0, scalar2=0.0, op0=ALU.add, op1=ALU.max)
+
+        def roots(u):
+            tile_no = place[u][0]
+            if tile_no not in a_of:
+                a_of[tile_no] = a_pool.tile([P, 4 * BANK], F32, name="a", tag="a")
+            a = a_of[tile_no]
+            x = x_of[tile_no]
+            c = columns(u)
+            if u < SCALAR_CLIPS:
+                nc.scalar.activation(out=x[:, c], in_=x[:, c], func=ACT.Relu, bias=minus_one[:, 0:1])
+            nc.scalar.activation(out=a[:, c], in_=x[:, c], func=ACT.Sqrt, bias=one[:, 0:1], scale=0.5)
+            nc.scalar.activation(out=x[:, c], in_=x[:, c], func=ACT.Sqrt, bias=floor_b[:, 0:1], scale=0.5)
+
+        def add_roots(u):
+            tile_no = place[u][0]
+            c = columns(u)
+            nc.vector.tensor_tensor(out=a_of[tile_no][:, c], in0=a_of[tile_no][:, c], in1=x_of[tile_no][:, c], op=ALU.add)
+
+        def logarithm(u):
+            a = a_of[place[u][0]]
+            c = columns(u)
+            nc.scalar.activation(out=a[:, c], in_=a[:, c], func=ACT.Ln)
+
+        def finish(u):
+            a = a_of[place[u][0]]
+            c = columns(u)
+            nc.vector.scalar_tensor_tensor(
+                out=a[:, c], in0=a[:, c], scalar=minus_4tau[:, 0:1], in1=a[:, c], op0=ALU.mult, op1=ALU.mult
+            )
+            banks = units[u]
+            i0, h0 = banks[0]
+            if len(banks) > 1 and all(h == h0 for (i, h) in banks):
+                nc.sync.dma_start(
+                    out=out_tiles[:, i0 : i0 + len(banks), h0 * BANK : (h0 + 1) * BANK],
+                    in_=a[:, c].rearrange("p (i c) -> p i c", c=BANK),
+                )
+            else:
+                start = i0 * VOCAB + h0 * BANK
+                nc.sync.dma_start(out=out_flat[:, start : start + len(banks) * BANK], in_=a[:, c])
+
+        def group_of(u):
+            return max(i // GROUP for (i, h) in units[u])
+
+        queue = []
+        sanitised = 0
+        second_side = False
+        for u in range(n_units):
+            if not second_side and any(h == 1 for (i, h) in units[u]):
+                queue.append(("w_side", 1, 1))
+                second_side = True
+            if sanitised < group_of(u):
+                upto = sanitised + 1 if sanitised == 0 else sanitised + 2
+                queue.append(("sanitise", sanitised + 1, upto + 1))
+                sanitised = upto
+            queue.append(("x", u, u))
+        for r in range(SANITISE_LEAD):
+            k = 1
+            while k < len(queue):
+                if queue[k][0] == "sanitise" and queue[k - 1][0] != "sanitise":
+                    queue[k - 1], queue[k] = queue[k], queue[k - 1]
+                    k += 1
+                k += 1
+
+        state = {"sanitised": 0, "turned": 0, "quantised": 0, "step": 0, "late_t": False, "next": 0}
+        sanitise_step = {}
+        turn_step = {}
+        x_made = set()
+
+        def turn(g):
+            h_transpose(g)
+            h_copy_out(g)
+            state["turned"] = g
+            turn_step[g] = state["step"]
+
+        def quantise(g):
+            h_quantise(g)
+            state["quantised"] = g
+
+        def pull():
+            kind, n, m = queue[state["next"]]
+            state["next"] += 1
+            if kind == "w_side":
+                w_side(n)
+            elif kind == "sanitise":
+                sanitise_factor(n, m)
+                sanitise_apply(n, m)
+                state["sanitised"] = m - 1
+                for g in range(n, m):
+                    sanitise_step[g] = state["step"]
+            else:
+                g = group_of(n)
+                while state["turned"] < g:
+                    turn(state["turned"] + 1)
+                while state["quantised"] < g:
+                    quantise(state["quantised"] + 1)
+                if not state["late_t"] and any(i >= CHUNK for (i, h) in units[n]):
+                    time_coordinates(1, TILES // CHUNK)
+                    state["late_t"] = True
+                dot(n)
+                make_x(n)
+                x_made.add(n)
+
+        def pull_until(u):
+            while u not in x_made:
+                pull()
+
+        def advance():
+            state["step"] += 1
+            while state["quantised"] < state["turned"] and turn_step[state["quantised"] + 1] + QUANTISE_LAG <= state["step"]:
+                quantise(state["quantised"] + 1)
+            while state["turned"] < state["sanitised"] and sanitise_step[state["turned"] + 1] + TRANSPOSE_LAG <= state["step"]:
+                turn(state["turned"] + 1)
+
+        for k in range(FIRST_PULLS):
+            pull()
+        batch_start = 0
+        for size in BATCHES:
+            for u in range(batch_start, batch_start + size):
+                pull_until(u)
+                advance()
+                roots(u)
+                pull_until(min(n_units - 1, u + LOOKAHEAD))
+                add_roots(u)
+            for u in range(batch_start, batch_start + size):
+                advance()
+                logarithm(u)
+                finish(u)
+            batch_start += size

@@ -34,7 +34,8 @@ A_TILES = 9
 SANITISE_LEAD = 4
 TRANSPOSE_LAG = 2
 QUANTISE_LAG = 1
-SCALAR_CLIPS = 7
+X_MIN = 1.0 + 2.0**-23
+X_MAX = 3.4028234663852886e38
 FIRST_PULLS = 3
 
 
@@ -70,15 +71,15 @@ def tile_geodesiclmheadv2_t_kernel(tc, hidden_states, weight, logit_scale, out):
 
         ident = keep.tile([P, P], F32, name="ident")
         one = keep.tile([P, 1], F32, name="one")
-        minus_one = keep.tile([P, 1], F32, name="minus_one")
-        floor_b = keep.tile([P, 1], F32, name="floor_b")
+        half = keep.tile([P, 1], F32, name="half")
+        minus_half = keep.tile([P, 1], F32, name="minus_half")
         scratch = keep.tile([P, 1], F32, name="scratch")
         ident_bf = keep.tile([P, P], BF16, name="ident_bf")
         make_identity(nc, ident[:])
         make_identity(nc, ident_bf[:])
         nc.vector.memset(one[:], 1.0)
-        nc.vector.memset(minus_one[:], -1.0)
-        nc.vector.memset(floor_b[:], 0.5e-12)
+        nc.vector.memset(half[:], 0.5)
+        nc.vector.memset(minus_half[:], -0.5)
         nc.scalar.activation(out=scratch[:], in_=one[:], func=ACT.Sqrt)
 
         w_raw = [keep.tile([P, 2 * K], BF16, name="w_raw%d" % q) for q in range(W_TILES // 2)]
@@ -358,9 +359,8 @@ def tile_geodesiclmheadv2_t_kernel(tc, hidden_states, weight, logit_scale, out):
                     op0=ALU.mult,
                     op1=ALU.subtract,
                 )
-            if u >= SCALAR_CLIPS:
-                c = columns(u)
-                nc.vector.tensor_scalar(out=x[:, c], in0=x[:, c], scalar1=-1.0, scalar2=0.0, op0=ALU.add, op1=ALU.max)
+            c = columns(u)
+            nc.gpsimd.tensor_scalar(out=x[:, c], in0=x[:, c], scalar1=X_MAX, scalar2=X_MIN, op0=ALU.min, op1=ALU.max)
 
         def roots(u):
             tile_no = place[u][0]
@@ -369,10 +369,8 @@ def tile_geodesiclmheadv2_t_kernel(tc, hidden_states, weight, logit_scale, out):
             a = a_of[tile_no]
             x = x_of[tile_no]
             c = columns(u)
-            if u < SCALAR_CLIPS:
-                nc.scalar.activation(out=x[:, c], in_=x[:, c], func=ACT.Relu, bias=minus_one[:, 0:1])
-            nc.scalar.activation(out=a[:, c], in_=x[:, c], func=ACT.Sqrt, bias=one[:, 0:1], scale=0.5)
-            nc.scalar.activation(out=x[:, c], in_=x[:, c], func=ACT.Sqrt, bias=floor_b[:, 0:1], scale=0.5)
+            nc.scalar.activation(out=a[:, c], in_=x[:, c], func=ACT.Sqrt, bias=half[:, 0:1], scale=0.5)
+            nc.scalar.activation(out=x[:, c], in_=x[:, c], func=ACT.Sqrt, bias=minus_half[:, 0:1], scale=0.5)
 
         def add_roots(u):
             tile_no = place[u][0]

@@ -25,40 +25,22 @@ SLOT = 528
 FMAX = 3.3895313892515355e38
 C_INF = 1.0e4 / FMAX
 SUMSQ_MAX = 7.0e3
-FLOPS = 2 * TOKENS * VOCAB * K
-
-BATCHES = (10, 10)
-LOOKAHEAD = 4
-X_TILES = 5
-A_TILES = 9
-SANITISE_LEAD = 4
-TRANSPOSE_LAG = 2
-QUANTISE_LAG = 1
 X_MIN = 1.0 + 2.0**-23
 X_MAX = 3.4028234663852886e38
-FIRST_PULLS = 3
+FLOPS = 2 * TOKENS * VOCAB * K
 
-
-def make_units():
-    units = [[(0, 0)], [(1, 0)], [(2, 0), (3, 0)], [(i, 1) for i in range(GROUP)]]
-    place = [(0, 0), (0, 1), (0, 2), (1, 0)]
-    for i in range(GROUP, TILES - 2, 2):
-        place.append((len(units) - 2, 0))
-        units.append([(i, 0), (i, 1), (i + 1, 0), (i + 1, 1)])
-    last = len(units) - 2
-    units.extend([[(TILES - 2, 0), (TILES - 2, 1)], [(TILES - 1, 0)], [(TILES - 1, 1)]])
-    place.extend([(last, 0), (last, 2), (last, 3)])
-    return units, place
+UNITS = TILES // 2
+BATCHES = (6, 5, 5)
+X_TILES = 6
+A_TILES = 8
+PACE = 16
 
 
 def tile_geodesiclmheadv2_t_kernel(tc, hidden_states, weight, logit_scale, out):
     nc = tc.nc
     hid = hidden_states.flatten_outer_dims().rearrange("(p i) c -> p i c", i=TILES)
-    out_tiles = out.flatten_outer_dims().rearrange("(p i) v -> p i v", i=TILES)
     out_flat = out.flatten_outer_dims().rearrange("(p i) v -> p (i v)", i=TILES)
     w_rows = weight.rearrange("(j p) k -> p j k", p=P)
-    units, place = make_units()
-    n_units = len(units)
 
     with ExitStack() as ctx:
         keep = ctx.enter_context(tc.tile_pool(name="keep", bufs=1))
@@ -75,27 +57,33 @@ def tile_geodesiclmheadv2_t_kernel(tc, hidden_states, weight, logit_scale, out):
         minus_half = keep.tile([P, 1], F32, name="minus_half")
         scratch = keep.tile([P, 1], F32, name="scratch")
         ident_bf = keep.tile([P, P], BF16, name="ident_bf")
-        make_identity(nc, ident[:])
-        make_identity(nc, ident_bf[:])
         nc.vector.memset(one[:], 1.0)
         nc.vector.memset(half[:], 0.5)
         nc.vector.memset(minus_half[:], -0.5)
         nc.scalar.activation(out=scratch[:], in_=one[:], func=ACT.Sqrt)
 
         w_raw = [keep.tile([P, 2 * K], BF16, name="w_raw%d" % q) for q in range(W_TILES // 2)]
+        h_raw = [keep.tile([P, CHUNK * SLOT], BF16, name="h_raw%d" % c) for c in range(TILES // CHUNK)]
+        scale_raw = keep.tile([P, 1], BF16, name="scale_raw")
+
+        def h_load(i0, i1):
+            c, first = i0 // CHUNK, i0 % CHUNK
+            nc.sync.dma_start(
+                out=h_raw[c][:].rearrange("p (i c) -> p i c", c=SLOT)[:, first : first + i1 - i0, 1 : K + 2],
+                in_=hid[:, i0:i1, :],
+            )
+
+        h_load(0, GROUP)
         for q in range(W_TILES // 2):
             nc.sync.dma_start(
                 out=w_raw[q][:].rearrange("p (j k) -> p j k", k=K), in_=w_rows[:, 2 * q : 2 * q + 2, :]
             )
-        h_raw = [keep.tile([P, CHUNK * SLOT], BF16, name="h_raw%d" % c) for c in range(TILES // CHUNK)]
-        scale_raw = keep.tile([P, 1], BF16, name="scale_raw")
-        for c in range(TILES // CHUNK):
-            nc.sync.dma_start(
-                out=h_raw[c][:].rearrange("p (i c) -> p i c", c=SLOT)[:, :, 1 : K + 2],
-                in_=hid[:, CHUNK * c : CHUNK * (c + 1), :],
-            )
-            if c == 0:
-                nc.sync.dma_start(out=scale_raw[:], in_=logit_scale.partition_broadcast(P))
+        h_load(GROUP, CHUNK)
+        nc.sync.dma_start(out=scale_raw[:], in_=logit_scale.partition_broadcast(P))
+        for c in range(1, TILES // CHUNK):
+            h_load(CHUNK * c, CHUNK * (c + 1))
+        make_identity(nc, ident[:])
+        make_identity(nc, ident_bf[:])
 
         def nan_to_num_factor(eng, up, down, x):
             eng.tensor_scalar(out=up, in0=x, scalar1=FMAX, scalar2=C_INF, op0=ALU.is_le, op1=ALU.add)
@@ -130,6 +118,7 @@ def tile_geodesiclmheadv2_t_kernel(tc, hidden_states, weight, logit_scale, out):
         nc.gpsimd.tensor_scalar(out=neg[:], in0=scale_raw[:], scalar1=0.0, scalar2=-4.0, op0=ALU.is_lt, op1=ALU.mult)
         nc.gpsimd.tensor_tensor(out=not_neg[:], in0=not_neg[:], in1=neg[:], op=ALU.add)
         nc.gpsimd.tensor_tensor(out=minus_4tau[:], in0=tau[:], in1=not_neg[:], op=ALU.mult)
+        time_coordinates(1, TILES // CHUNK)
 
         h_codes = [keep.tile([P, GROUP * P], U32, name="h_codes%d" % g, align_bytes=64) for g in range(GROUPS)]
         h_scales = [keep.tile([P, GROUP * P], U8, name="h_scales%d" % g, align_bytes=64) for g in range(GROUPS)]
@@ -138,25 +127,20 @@ def tile_geodesiclmheadv2_t_kernel(tc, hidden_states, weight, logit_scale, out):
         grouped_of = {}
         turned_of = {}
 
-        def sanitise_factor(g0, g1):
+        def sanitise(g0, g1):
             n = (g1 - g0) * GROUP
             first = (g0 % 2) * GROUP
             x = h_raw[g0 // 2][:].rearrange("p (i c) -> p i c", c=SLOT)[:, first : first + n, 2 : K + 2]
-            up = factor_up[:, 0 : n * K].rearrange("p (i c) -> p i c", c=K)
-            down = factor_down[:, 0 : n * K].rearrange("p (i c) -> p i c", c=K)
-            nan_to_num_factor(nc.vector, up, down, x)
-
-        def sanitise_apply(g0, g1):
-            n = (g1 - g0) * GROUP
-            first = (g0 % 2) * GROUP
-            x = h_raw[g0 // 2][:].rearrange("p (i c) -> p i c", c=SLOT)[:, first : first + n, 2 : K + 2]
-            nc.vector.tensor_tensor(
-                out=factor_up[:, 0 : n * K], in0=factor_up[:, 0 : n * K], in1=factor_down[:, 0 : n * K], op=ALU.mult
-            )
-            nc.vector.tensor_scalar(out=x, in0=x, scalar1=-FMAX, scalar2=FMAX, op0=ALU.max, op1=ALU.min)
-            nc.vector.tensor_tensor(
-                out=x, in0=x, in1=factor_up[:, 0 : n * K].rearrange("p (i c) -> p i c", c=K), op=ALU.mult
-            )
+            up, down = factor_up[:, 0 : n * K], factor_down[:, 0 : n * K]
+            up3 = up.rearrange("p (i c) -> p i c", c=K)
+            down3 = down.rearrange("p (i c) -> p i c", c=K)
+            return [
+                lambda: nc.vector.tensor_scalar(out=up3, in0=x, scalar1=FMAX, scalar2=C_INF, op0=ALU.is_le, op1=ALU.add),
+                lambda: nc.vector.tensor_scalar(out=down3, in0=x, scalar1=-FMAX, scalar2=C_INF, op0=ALU.is_ge, op1=ALU.add),
+                lambda: nc.vector.tensor_scalar(out=x, in0=x, scalar1=-FMAX, scalar2=FMAX, op0=ALU.max, op1=ALU.min),
+                lambda: nc.vector.tensor_tensor(out=up, in0=up, in1=down, op=ALU.mult),
+                lambda: nc.vector.tensor_tensor(out=x, in0=x, in1=up3, op=ALU.mult),
+            ]
 
         def h_transpose(g):
             for pair in range(2):
@@ -185,83 +169,37 @@ def tile_geodesiclmheadv2_t_kernel(tc, hidden_states, weight, logit_scale, out):
         def h_quantise(g):
             nc.vector.quantize_mx(out=h_codes[g][:].bitcast(FP8X4), scales=h_scales[g][:], in_=grouped_of[g][:])
 
-        sumsq_s = keep.tile([P, W_TILES], F32, name="sumsq_s")
         sumsq = keep.tile([P, W_TILES], F32, name="sumsq")
-        squares_s = keep.tile([P, K], BF16, name="squares_s")
-        squares_v = keep.tile([P, K], F32, name="squares_v")
-
-        def w_row_tile(j):
-            return w_raw[j // 2][:, (j % 2) * K : (j % 2 + 1) * K]
-
-        for j in (0, 1, 4, 5):
-            nc.scalar.activation(out=squares_s[:], in_=w_row_tile(j), func=ACT.Square, accum_out=sumsq_s[:, j : j + 1])
-        for j in (2, 3, 6, 7):
-            nc.vector.scalar_tensor_tensor(
-                out=squares_v[:], in0=w_row_tile(j), scalar=1.0, in1=w_row_tile(j), op0=ALU.mult, op1=ALU.mult,
-                accum_out=sumsq[:, j : j + 1],
-            )
-        nc.vector.tensor_copy(
-            out=sumsq[:].rearrange("p (a b) -> p a b", b=4)[:, :, 0:2],
-            in_=sumsq_s[:].rearrange("p (a b) -> p a b", b=4)[:, :, 0:2],
-        )
+        squares = keep.tile([P, K], BF16, name="squares")
         row_ok = keep.tile([P, W_TILES], F32, name="row_ok")
-        nc.vector.tensor_single_scalar(out=row_ok[:], in_=sumsq[:], scalar=FMAX, op=ALU.is_le)
-        nc.vector.tensor_scalar(out=sumsq[:], in0=sumsq[:], scalar1=1.0e-30, scalar2=SUMSQ_MAX, op0=ALU.max, op1=ALU.min)
-
         norm = keep.tile([P, W_TILES], F32, name="norm")
         e_plus = keep.tile([P, W_TILES], F32, name="e_plus")
         e_minus = keep.tile([P, W_TILES], F32, name="e_minus")
-        nc.scalar.activation(out=norm[:], in_=sumsq[:], func=ACT.Sqrt)
-        nc.scalar.activation(out=e_plus[:], in_=norm[:], func=ACT.Exp)
-        nc.scalar.activation(out=e_minus[:], in_=norm[:], func=ACT.Exp, scale=-1.0)
-        nc.scalar.activation(out=scratch[:], in_=one[:], func=ACT.Sqrt)
-
-        floor_n = keep.tile([P, W_TILES], F32, name="floor_n")
-        slope = keep.tile([P, W_TILES], F32, name="slope")
-        offset = keep.tile([P, W_TILES], F32, name="offset")
-        large = keep.tile([P, W_TILES], F32, name="large")
+        inverse = keep.tile([P, W_TILES], F32, name="inverse")
         diff = keep.tile([P, W_TILES], F32, name="diff")
         total = keep.tile([P, W_TILES], F32, name="total")
         r_col = keep.tile([P, W_TILES], F32, name="r_col")
         cosh_col = keep.tile([P, W_TILES], F32, name="cosh_col")
-        nc.vector.tensor_scalar_max(out=floor_n[:], in0=norm[:], scalar1=1.0e-7)
-        nc.vector.reciprocal(out=slope[:], in_=floor_n[:])
-        nc.vector.tensor_single_scalar(out=large[:], in_=norm[:], scalar=1.0e-7, op=ALU.is_gt)
-        nc.vector.scalar_tensor_tensor(out=slope[:], in0=slope[:], scalar=0.5, in1=large[:], op0=ALU.mult, op1=ALU.mult)
-        nc.vector.tensor_tensor(out=slope[:], in0=slope[:], in1=row_ok[:], op=ALU.mult)
-        nc.vector.scalar_tensor_tensor(out=offset[:], in0=large[:], scalar=-1.0, in1=row_ok[:], op0=ALU.mult, op1=ALU.add)
-        nc.vector.tensor_scalar_max(out=offset[:], in0=offset[:], scalar1=0.0)
-        for q in range(W_TILES // 2):
-            nc.vector.tensor_scalar(out=w_raw[q][:], in0=w_raw[q][:], scalar1=-FMAX, scalar2=FMAX, op0=ALU.max, op1=ALU.min)
 
-        sanitise_factor(0, 1)
-        nc.vector.tensor_tensor(out=diff[:], in0=e_plus[:], in1=e_minus[:], op=ALU.subtract)
-        nc.vector.tensor_tensor(out=diff[:], in0=diff[:], in1=slope[:], op=ALU.mult)
-        nc.vector.tensor_tensor(out=r_col[:], in0=diff[:], in1=offset[:], op=ALU.add)
-        sanitise_apply(0, 1)
-        nc.vector.tensor_tensor(out=total[:], in0=e_plus[:], in1=e_minus[:], op=ALU.add)
-        nc.vector.scalar_tensor_tensor(out=cosh_col[:], in0=total[:], scalar=0.5, in1=row_ok[:], op0=ALU.mult, op1=ALU.mult)
+        def w_row_tile(j):
+            return w_raw[j // 2][:, (j % 2) * K : (j % 2 + 1) * K]
 
         cosh_row = keep.tile([P, VOCAB], F32, name="cosh_row")
         spread_of = {}
 
-        def spread(column, key):
-            h = key[1]
+        def spread(h):
             bank = sum_pool.tile([P, BANK], F32, name="spread", tag="sum")
-            spread_of[key] = bank
+            spread_of[h] = bank
             for jj in range(4):
                 j = 4 * h + jj
-                nc.tensor.matmul(
+                nc.tensor.transpose(
                     out=bank[:, jj * P : (jj + 1) * P],
-                    lhsT=column[:, j : j + 1].to_broadcast([P, P]),
-                    rhs=ident[:],
-                    start=True,
-                    stop=True,
+                    in_=cosh_col[:, j : j + 1].to_broadcast([P, P]),
+                    identity=ident[:],
                 )
 
-        def spread_copy(row, key):
-            h = key[1]
-            nc.scalar.copy(out=row[:, h * BANK : (h + 1) * BANK], in_=spread_of[key][:])
+        def spread_copy(h):
+            nc.scalar.copy(out=cosh_row[:, h * BANK : (h + 1) * BANK], in_=spread_of[h][:])
 
         w_space = keep.tile([P, W_TILES * K], BF16, name="w_space")
         w_grouped = [keep.tile([P, 4 * BANK], BF16, name="w_grouped%d" % h, align_bytes=64) for h in range(2)]
@@ -303,34 +241,13 @@ def tile_geodesiclmheadv2_t_kernel(tc, hidden_states, weight, logit_scale, out):
                 in_=w_grouped[h][:],
             )
 
-        def w_side(h):
-            for j in range(4 * h, 4 * h + 4):
-                w_scale(j)
-            w_transpose(2 * h)
-            w_transpose(2 * h + 1)
-            if h == 0:
-                h_transpose(0)
-            spread(cosh_col, ("cosh", h))
-            w_copy_out(2 * h)
-            w_copy_out(2 * h + 1)
-            if h == 0:
-                h_copy_out(0)
-            spread_copy(cosh_row, ("cosh", h))
-            w_quantise(h)
-
-        w_side(0)
-        h_quantise(0)
-
         dot_of = {}
         x_of = {}
         a_of = {}
 
-        def columns(u):
-            first = place[u][1] * BANK
-            return slice(first, first + len(units[u]) * BANK)
-
         def dot(u):
-            for k, (i, h) in enumerate(units[u]):
+            for k in range(4):
+                i, h = 2 * u + k // 2, k % 2
                 g = i // GROUP
                 tokens = slice((i % GROUP) * P, (i % GROUP + 1) * P)
                 bank = sum_pool.tile([P, BANK], F32, name="dot", tag="sum")
@@ -346,144 +263,120 @@ def tile_geodesiclmheadv2_t_kernel(tc, hidden_states, weight, logit_scale, out):
                 )
 
         def make_x(u):
-            tile_no, first = place[u]
-            if tile_no not in x_of:
-                x_of[tile_no] = x_pool.tile([P, 4 * BANK], F32, name="x", tag="x")
-            x = x_of[tile_no]
-            for k, (i, h) in enumerate(units[u]):
+            x_of[u] = x_pool.tile([P, 4 * BANK], F32, name="x", tag="x")
+            for k in range(4):
+                i, h = 2 * u + k // 2, k % 2
                 nc.vector.scalar_tensor_tensor(
-                    out=x[:, (first + k) * BANK : (first + k + 1) * BANK],
+                    out=x_of[u][:, k * BANK : (k + 1) * BANK],
                     in0=cosh_row[:, h * BANK : (h + 1) * BANK],
                     scalar=t_coord[:, i : i + 1],
                     in1=dot_of[(u, k)][:],
                     op0=ALU.mult,
                     op1=ALU.subtract,
                 )
-            c = columns(u)
-            nc.gpsimd.tensor_scalar(out=x[:, c], in0=x[:, c], scalar1=X_MAX, scalar2=X_MIN, op0=ALU.min, op1=ALU.max)
+
+        def clip(eng, u, c0=0, c1=4 * BANK):
+            x = x_of[u][:, c0:c1]
+            eng.tensor_scalar(out=x, in0=x, scalar1=X_MAX, scalar2=X_MIN, op0=ALU.min, op1=ALU.max)
 
         def roots(u):
-            tile_no = place[u][0]
-            if tile_no not in a_of:
-                a_of[tile_no] = a_pool.tile([P, 4 * BANK], F32, name="a", tag="a")
-            a = a_of[tile_no]
-            x = x_of[tile_no]
-            c = columns(u)
-            nc.scalar.activation(out=a[:, c], in_=x[:, c], func=ACT.Sqrt, bias=half[:, 0:1], scale=0.5)
-            nc.scalar.activation(out=x[:, c], in_=x[:, c], func=ACT.Sqrt, bias=minus_half[:, 0:1], scale=0.5)
+            a_of[u] = a_pool.tile([P, 4 * BANK], F32, name="a", tag="a")
+            nc.scalar.activation(out=a_of[u][:], in_=x_of[u][:], func=ACT.Sqrt, bias=half[:, 0:1], scale=0.5)
+            nc.scalar.activation(out=x_of[u][:], in_=x_of[u][:], func=ACT.Sqrt, bias=minus_half[:, 0:1], scale=0.5)
 
         def add_roots(u):
-            tile_no = place[u][0]
-            c = columns(u)
-            nc.vector.tensor_tensor(out=a_of[tile_no][:, c], in0=a_of[tile_no][:, c], in1=x_of[tile_no][:, c], op=ALU.add)
+            nc.vector.tensor_tensor(out=a_of[u][:], in0=a_of[u][:], in1=x_of[u][:], op=ALU.add)
 
-        def logarithm(u):
-            a = a_of[place[u][0]]
-            c = columns(u)
-            nc.scalar.activation(out=a[:, c], in_=a[:, c], func=ACT.Ln)
+        def logarithm(u, c0=0, c1=4 * BANK):
+            nc.scalar.activation(out=a_of[u][:, c0:c1], in_=a_of[u][:, c0:c1], func=ACT.Ln)
 
-        def finish(u):
-            a = a_of[place[u][0]]
-            c = columns(u)
-            nc.vector.scalar_tensor_tensor(
-                out=a[:, c], in0=a[:, c], scalar=minus_4tau[:, 0:1], in1=a[:, c], op0=ALU.mult, op1=ALU.mult
-            )
-            banks = units[u]
-            i0, h0 = banks[0]
-            if len(banks) > 1 and all(h == h0 for (i, h) in banks):
-                nc.sync.dma_start(
-                    out=out_tiles[:, i0 : i0 + len(banks), h0 * BANK : (h0 + 1) * BANK],
-                    in_=a[:, c].rearrange("p (i c) -> p i c", c=BANK),
-                )
-            else:
-                start = i0 * VOCAB + h0 * BANK
-                nc.sync.dma_start(out=out_flat[:, start : start + len(banks) * BANK], in_=a[:, c])
+        def finish(u, c0=0, c1=4 * BANK):
+            a = a_of[u][:, c0:c1]
+            nc.vector.scalar_tensor_tensor(out=a, in0=a, scalar=minus_4tau[:, 0:1], in1=a, op0=ALU.mult, op1=ALU.mult)
+            nc.sync.dma_start(out=out_flat[:, 4 * BANK * u + c0 : 4 * BANK * u + c1], in_=a)
 
-        def group_of(u):
-            return max(i // GROUP for (i, h) in units[u])
+        first_half = sanitise(0, 1)
+        for step in first_half:
+            step()
+        for j in range(W_TILES):
+            nc.scalar.activation(out=squares[:], in_=w_row_tile(j), func=ACT.Square, accum_out=sumsq[:, j : j + 1])
+        h_transpose(0)
+        second_half = sanitise(1, 2)
+        for q in range(2):
+            nc.vector.tensor_scalar(out=w_raw[q][:], in0=w_raw[q][:], scalar1=-FMAX, scalar2=FMAX, op0=ALU.max, op1=ALU.min)
+        second_half[0]()
+        second_half[1]()
+        nc.vector.tensor_single_scalar(out=row_ok[:], in_=sumsq[:], scalar=FMAX, op=ALU.is_le)
+        nc.vector.tensor_scalar(out=sumsq[:], in0=sumsq[:], scalar1=1.0e-30, scalar2=SUMSQ_MAX, op0=ALU.max, op1=ALU.min)
+        second_half[2]()
+        second_half[3]()
+        nc.scalar.activation(out=norm[:], in_=sumsq[:], func=ACT.Sqrt)
+        nc.scalar.activation(out=e_plus[:], in_=norm[:], func=ACT.Exp)
+        nc.scalar.activation(out=e_minus[:], in_=norm[:], func=ACT.Exp, scale=-1.0)
+        h_copy_out(0)
+        nc.scalar.activation(out=scratch[:], in_=one[:], func=ACT.Sqrt)
+        nc.vector.reciprocal(out=inverse[:], in_=norm[:])
+        for q in range(2, 4):
+            nc.vector.tensor_scalar(out=w_raw[q][:], in0=w_raw[q][:], scalar1=-FMAX, scalar2=FMAX, op0=ALU.max, op1=ALU.min)
+        nc.vector.tensor_tensor(out=diff[:], in0=e_plus[:], in1=e_minus[:], op=ALU.subtract)
+        nc.vector.tensor_tensor(out=total[:], in0=e_plus[:], in1=e_minus[:], op=ALU.add)
+        nc.vector.scalar_tensor_tensor(out=diff[:], in0=diff[:], scalar=0.5, in1=inverse[:], op0=ALU.mult, op1=ALU.mult)
+        nc.vector.scalar_tensor_tensor(out=cosh_col[:], in0=total[:], scalar=0.5, in1=row_ok[:], op0=ALU.mult, op1=ALU.mult)
+        nc.vector.scalar_tensor_tensor(out=r_col[:], in0=diff[:], scalar=1.0, in1=row_ok[:], op0=ALU.max, op1=ALU.mult)
+        second_half[4]()
+        h_quantise(0)
+        for step in sanitise(2, 4):
+            step()
+        for h in range(2):
+            for j in range(4 * h, 4 * h + 4):
+                w_scale(j)
+            w_transpose(2 * h)
+            w_transpose(2 * h + 1)
+            spread(h)
+            w_copy_out(2 * h)
+            w_copy_out(2 * h + 1)
+            spread_copy(h)
+            w_quantise(h)
+        h_transpose(1)
+        h_copy_out(1)
+        h_quantise(1)
+        late = sanitise(4, 6) + sanitise(6, 8)
 
-        queue = []
-        sanitised = 0
-        second_side = False
-        for u in range(n_units):
-            if not second_side and any(h == 1 for (i, h) in units[u]):
-                queue.append(("w_side", 1, 1))
-                second_side = True
-            if sanitised < group_of(u):
-                upto = sanitised + 1 if sanitised == 0 else sanitised + 2
-                queue.append(("sanitise", sanitised + 1, upto + 1))
-                sanitised = upto
-            queue.append(("x", u, u))
-        for r in range(SANITISE_LEAD):
-            k = 1
-            while k < len(queue):
-                if queue[k][0] == "sanitise" and queue[k - 1][0] != "sanitise":
-                    queue[k - 1], queue[k] = queue[k], queue[k - 1]
-                    k += 1
-                k += 1
-
-        state = {"sanitised": 0, "turned": 0, "quantised": 0, "step": 0, "late_t": False, "next": 0}
-        sanitise_step = {}
-        turn_step = {}
-        x_made = set()
-
-        def turn(g):
-            h_transpose(g)
-            h_copy_out(g)
-            state["turned"] = g
-            turn_step[g] = state["step"]
-
-        def quantise(g):
-            h_quantise(g)
-            state["quantised"] = g
-
-        def pull():
-            kind, n, m = queue[state["next"]]
-            state["next"] += 1
-            if kind == "w_side":
-                w_side(n)
-            elif kind == "sanitise":
-                sanitise_factor(n, m)
-                sanitise_apply(n, m)
-                state["sanitised"] = m - 1
-                for g in range(n, m):
-                    sanitise_step[g] = state["step"]
-            else:
-                g = group_of(n)
-                while state["turned"] < g:
-                    turn(state["turned"] + 1)
-                while state["quantised"] < g:
-                    quantise(state["quantised"] + 1)
-                if not state["late_t"] and any(i >= CHUNK for (i, h) in units[n]):
-                    time_coordinates(1, TILES // CHUNK)
-                    state["late_t"] = True
-                dot(n)
-                make_x(n)
-                x_made.add(n)
-
-        def pull_until(u):
-            while u not in x_made:
-                pull()
-
-        def advance():
-            state["step"] += 1
-            while state["quantised"] < state["turned"] and turn_step[state["quantised"] + 1] + QUANTISE_LAG <= state["step"]:
-                quantise(state["quantised"] + 1)
-            while state["turned"] < state["sanitised"] and sanitise_step[state["turned"] + 1] + TRANSPOSE_LAG <= state["step"]:
-                turn(state["turned"] + 1)
-
-        for k in range(FIRST_PULLS):
-            pull()
-        batch_start = 0
+        last = None
+        first = 0
+        previous = []
+        turned = 2
         for size in BATCHES:
-            for u in range(batch_start, batch_start + size):
-                pull_until(u)
-                advance()
-                roots(u)
-                pull_until(min(n_units - 1, u + LOOKAHEAD))
-                add_roots(u)
-            for u in range(batch_start, batch_start + size):
-                advance()
-                logarithm(u)
+            batch = list(range(first, first + size))
+            first += size
+            for k, u in enumerate(batch):
+                g = (2 * u + 1) // GROUP
+                dot(u)
+                make_x(u)
+                if k > 0:
+                    clip(nc.gpsimd, u, 0, PACE)
+                    clip(nc.gpsimd, u - 1, PACE if k > 1 else 0, 4 * BANK)
+                if k == size - 1:
+                    clip(nc.vector, u, PACE, 4 * BANK)
+                if previous:
+                    finish(previous.pop(0))
+                for step in late[:3]:
+                    step()
+                late = late[3:]
+                if u % 2 == 0 and turned < GROUPS:
+                    h_transpose(turned)
+                    h_copy_out(turned)
+                    turned += 1
+                if k > 0:
+                    roots(u - 1)
+                if u % 2 == 1 and g + 1 < turned:
+                    h_quantise(g + 1)
+            roots(batch[-1])
+            for u in previous:
                 finish(u)
-            batch_start += size
+            for u in batch:
+                add_roots(u)
+                logarithm(u)
+            previous = list(batch)
+        for u in previous:
+            finish(u)

@@ -30,10 +30,12 @@ X_MAX = 3.4028234663852886e38
 FLOPS = 2 * TOKENS * VOCAB * K
 
 UNITS = TILES // 2
-BATCHES = (6, 5, 5)
-X_TILES = 6
-A_TILES = 8
-PACE = 16
+BATCHES = (8, 8)
+X_TILES = 8
+A_TILES = 9
+SCALAR_CLIPS = (0, 1, 2, 3)
+EARLY_SUMS = (8,)
+LATE_SUMS = (9,)
 
 
 def tile_geodesiclmheadv2_t_kernel(tc, hidden_states, weight, logit_scale, out):
@@ -58,11 +60,16 @@ def tile_geodesiclmheadv2_t_kernel(tc, hidden_states, weight, logit_scale, out):
         scratch = keep.tile([P, 1], F32, name="scratch")
         ident_bf = keep.tile([P, P], BF16, name="ident_bf")
         nc.vector.memset(one[:], 1.0)
+        minus_one = keep.tile([P, 1], F32, name="minus_one")
+        floor_b = keep.tile([P, 1], F32, name="floor_b")
+        nc.vector.memset(minus_one[:], -1.0)
+        nc.vector.memset(floor_b[:], 0.5e-12)
         nc.vector.memset(half[:], 0.5)
         nc.vector.memset(minus_half[:], -0.5)
         nc.scalar.activation(out=scratch[:], in_=one[:], func=ACT.Sqrt)
 
-        w_raw = [keep.tile([P, 2 * K], BF16, name="w_raw%d" % q) for q in range(W_TILES // 2)]
+        w_rows_tile = x_pool.tile([P, 4 * BANK], F32, name="w_rows_tile", tag="x", align_bytes=64)
+        w_raw = [w_rows_tile[:, q * K : (q + 1) * K].bitcast(BF16) for q in range(W_TILES // 2)]
         h_raw = [keep.tile([P, CHUNK * SLOT], BF16, name="h_raw%d" % c) for c in range(TILES // CHUNK)]
         scale_raw = keep.tile([P, 1], BF16, name="scale_raw")
 
@@ -76,7 +83,7 @@ def tile_geodesiclmheadv2_t_kernel(tc, hidden_states, weight, logit_scale, out):
         h_load(0, GROUP)
         for q in range(W_TILES // 2):
             nc.sync.dma_start(
-                out=w_raw[q][:].rearrange("p (j k) -> p j k", k=K), in_=w_rows[:, 2 * q : 2 * q + 2, :]
+                out=w_raw[q].rearrange("p (j k) -> p j k", k=K), in_=w_rows[:, 2 * q : 2 * q + 2, :]
             )
         h_load(GROUP, CHUNK)
         nc.sync.dma_start(out=scale_raw[:], in_=logit_scale.partition_broadcast(P))
@@ -122,8 +129,10 @@ def tile_geodesiclmheadv2_t_kernel(tc, hidden_states, weight, logit_scale, out):
 
         h_codes = [keep.tile([P, GROUP * P], U32, name="h_codes%d" % g, align_bytes=64) for g in range(GROUPS)]
         h_scales = [keep.tile([P, GROUP * P], U8, name="h_scales%d" % g, align_bytes=64) for g in range(GROUPS)]
-        factor_up = keep.tile([P, CHUNK * K], BF16, name="factor_up")
-        factor_down = keep.tile([P, CHUNK * K], BF16, name="factor_down")
+        factor_up_tile = a_pool.tile([P, 4 * BANK], F32, name="factor_up_tile", tag="a")
+        factor_down_tile = a_pool.tile([P, 4 * BANK], F32, name="factor_down_tile", tag="a")
+        factor_up = factor_up_tile[:].bitcast(BF16)
+        factor_down = factor_down_tile[:].bitcast(BF16)
         grouped_of = {}
         turned_of = {}
 
@@ -201,8 +210,10 @@ def tile_geodesiclmheadv2_t_kernel(tc, hidden_states, weight, logit_scale, out):
         def spread_copy(h):
             nc.scalar.copy(out=cosh_row[:, h * BANK : (h + 1) * BANK], in_=spread_of[h][:])
 
-        w_space = keep.tile([P, W_TILES * K], BF16, name="w_space")
-        w_grouped = [keep.tile([P, 4 * BANK], BF16, name="w_grouped%d" % h, align_bytes=64) for h in range(2)]
+        w_space_tile = x_pool.tile([P, 4 * BANK], F32, name="w_space_tile", tag="x", align_bytes=64)
+        w_space = w_space_tile[:].bitcast(BF16)
+        w_grouped_tile = x_pool.tile([P, 4 * BANK], F32, name="w_grouped_tile", tag="x", align_bytes=64)
+        w_grouped = [w_grouped_tile[:, h * 2 * BANK : (h + 1) * 2 * BANK].bitcast(BF16) for h in range(2)]
         w_codes = keep.tile([P, VOCAB], U32, name="w_codes", align_bytes=64)
         w_scales = keep.tile([P, VOCAB], U8, name="w_scales", align_bytes=64)
         w_turned = {}
@@ -238,7 +249,7 @@ def tile_geodesiclmheadv2_t_kernel(tc, hidden_states, weight, logit_scale, out):
             nc.vector.quantize_mx(
                 out=w_codes[:, h * BANK : (h + 1) * BANK].bitcast(FP8X4),
                 scales=w_scales[:, h * BANK : (h + 1) * BANK],
-                in_=w_grouped[h][:],
+                in_=w_grouped[h],
             )
 
         dot_of = {}
@@ -263,7 +274,7 @@ def tile_geodesiclmheadv2_t_kernel(tc, hidden_states, weight, logit_scale, out):
                 )
 
         def make_x(u):
-            x_of[u] = x_pool.tile([P, 4 * BANK], F32, name="x", tag="x")
+            x_of[u] = x_pool.tile([P, 4 * BANK], F32, name="x", tag="x", align_bytes=64)
             for k in range(4):
                 i, h = 2 * u + k // 2, k % 2
                 nc.vector.scalar_tensor_tensor(
@@ -281,11 +292,29 @@ def tile_geodesiclmheadv2_t_kernel(tc, hidden_states, weight, logit_scale, out):
 
         def roots(u):
             a_of[u] = a_pool.tile([P, 4 * BANK], F32, name="a", tag="a")
+            if u in SCALAR_CLIPS:
+                nc.scalar.activation(out=x_of[u][:], in_=x_of[u][:], func=ACT.Relu, bias=minus_one[:, 0:1])
+                nc.scalar.activation(out=a_of[u][:], in_=x_of[u][:], func=ACT.Sqrt, bias=one[:, 0:1], scale=0.5)
+                nc.scalar.activation(out=x_of[u][:], in_=x_of[u][:], func=ACT.Sqrt, bias=floor_b[:, 0:1], scale=0.5)
+                return
             nc.scalar.activation(out=a_of[u][:], in_=x_of[u][:], func=ACT.Sqrt, bias=half[:, 0:1], scale=0.5)
             nc.scalar.activation(out=x_of[u][:], in_=x_of[u][:], func=ACT.Sqrt, bias=minus_half[:, 0:1], scale=0.5)
 
         def add_roots(u):
             nc.vector.tensor_tensor(out=a_of[u][:], in0=a_of[u][:], in1=x_of[u][:], op=ALU.add)
+
+        sum_of = {}
+
+        def sum_on_tensor(u, k):
+            c = slice(k * BANK, (k + 1) * BANK)
+            bank = turn_pool.tile([P, BANK], F32, name="root_sum", tag="turn")
+            sum_of[(u, k)] = bank
+            nc.tensor.matmul(out=bank[:], lhsT=ident[:], rhs=a_of[u][:, c], start=True, stop=False)
+            nc.tensor.matmul(out=bank[:], lhsT=ident[:], rhs=x_of[u][:, c], start=False, stop=True)
+
+        def logarithm_of_sum(u, k):
+            c = slice(k * BANK, (k + 1) * BANK)
+            nc.scalar.activation(out=a_of[u][:, c], in_=sum_of[(u, k)][:], func=ACT.Ln)
 
         def logarithm(u, c0=0, c1=4 * BANK):
             nc.scalar.activation(out=a_of[u][:, c0:c1], in_=a_of[u][:, c0:c1], func=ACT.Ln)
@@ -303,7 +332,7 @@ def tile_geodesiclmheadv2_t_kernel(tc, hidden_states, weight, logit_scale, out):
         h_transpose(0)
         second_half = sanitise(1, 2)
         for q in range(2):
-            nc.vector.tensor_scalar(out=w_raw[q][:], in0=w_raw[q][:], scalar1=-FMAX, scalar2=FMAX, op0=ALU.max, op1=ALU.min)
+            nc.vector.tensor_scalar(out=w_raw[q], in0=w_raw[q], scalar1=-FMAX, scalar2=FMAX, op0=ALU.max, op1=ALU.min)
         second_half[0]()
         second_half[1]()
         nc.vector.tensor_single_scalar(out=row_ok[:], in_=sumsq[:], scalar=FMAX, op=ALU.is_le)
@@ -317,7 +346,7 @@ def tile_geodesiclmheadv2_t_kernel(tc, hidden_states, weight, logit_scale, out):
         nc.scalar.activation(out=scratch[:], in_=one[:], func=ACT.Sqrt)
         nc.vector.reciprocal(out=inverse[:], in_=norm[:])
         for q in range(2, 4):
-            nc.vector.tensor_scalar(out=w_raw[q][:], in0=w_raw[q][:], scalar1=-FMAX, scalar2=FMAX, op0=ALU.max, op1=ALU.min)
+            nc.vector.tensor_scalar(out=w_raw[q], in0=w_raw[q], scalar1=-FMAX, scalar2=FMAX, op0=ALU.max, op1=ALU.min)
         nc.vector.tensor_tensor(out=diff[:], in0=e_plus[:], in1=e_minus[:], op=ALU.subtract)
         nc.vector.tensor_tensor(out=total[:], in0=e_plus[:], in1=e_minus[:], op=ALU.add)
         nc.vector.scalar_tensor_tensor(out=diff[:], in0=diff[:], scalar=0.5, in1=inverse[:], op0=ALU.mult, op1=ALU.mult)
@@ -340,43 +369,64 @@ def tile_geodesiclmheadv2_t_kernel(tc, hidden_states, weight, logit_scale, out):
         h_transpose(1)
         h_copy_out(1)
         h_quantise(1)
-        late = sanitise(4, 6) + sanitise(6, 8)
 
-        last = None
+        late = sanitise(4, 6) + sanitise(6, 8)
+        turned = 2
+
         first = 0
         previous = []
-        turned = 2
+        dot(0)
         for size in BATCHES:
             batch = list(range(first, first + size))
             first += size
+            early = [(u, k) for u in batch if u in EARLY_SUMS for k in range(4)]
+            late_sums = [(u, k) for u in batch if u in LATE_SUMS for k in range(4)]
+            summed = []
             for k, u in enumerate(batch):
-                g = (2 * u + 1) // GROUP
-                dot(u)
                 make_x(u)
-                if k > 0:
-                    clip(nc.gpsimd, u, 0, PACE)
-                    clip(nc.gpsimd, u - 1, PACE if k > 1 else 0, 4 * BANK)
-                if k == size - 1:
-                    clip(nc.vector, u, PACE, 4 * BANK)
+                if turned < GROUPS and True:
+                    h_transpose(turned)
+                if u + 1 < UNITS:
+                    dot(u + 1)
                 if previous:
                     finish(previous.pop(0))
-                for step in late[:3]:
+                if u not in SCALAR_CLIPS and not late:
+                    clip(nc.vector, u)
+                for step in late[:2]:
                     step()
-                late = late[3:]
-                if u % 2 == 0 and turned < GROUPS:
-                    h_transpose(turned)
+                if u not in SCALAR_CLIPS and late:
+                    clip(nc.vector, u)
+                late = late[2:]
+                if k > 1 and early:
+                    summed.append(early.pop(0))
+                    sum_on_tensor(*summed[-1])
+                if turned < GROUPS:
                     h_copy_out(turned)
-                    turned += 1
                 if k > 0:
                     roots(u - 1)
-                if u % 2 == 1 and g + 1 < turned:
-                    h_quantise(g + 1)
+                if turned < GROUPS:
+                    h_quantise(turned)
+                    turned += 1
+            while early:
+                summed.append(early.pop(0))
+                sum_on_tensor(*summed[-1])
             roots(batch[-1])
             for u in previous:
                 finish(u)
-            for u in batch:
+            for s in summed:
+                logarithm_of_sum(*s)
+                if late_sums:
+                    summed.append(late_sums.pop(0))
+                    sum_on_tensor(*summed[-1])
+                    if late_sums == []:
+                        break
+            others = [u for u in batch if u not in EARLY_SUMS + LATE_SUMS]
+            for u in others:
                 add_roots(u)
                 logarithm(u)
-            previous = list(batch)
+            for u, k in summed:
+                if u in LATE_SUMS:
+                    logarithm_of_sum(u, k)
+            previous = [u for u in batch if u in EARLY_SUMS] + others + [u for u in batch if u in LATE_SUMS]
         for u in previous:
             finish(u)

@@ -33,9 +33,14 @@ UNITS = TILES // 2
 BATCHES = (8, 8)
 X_TILES = 8
 A_TILES = 9
-SCALAR_CLIPS = (0, 1, 2, 3)
 EARLY_SUMS = (8,)
 LATE_SUMS = (9,)
+SCALAR_CLIPS = (0,)
+VECTOR_CLIPS = (7, 15)
+SQUARED = ()
+HEAD_A = 8
+HEAD_B = 8
+LATE_STEPS = 2
 
 
 def tile_geodesiclmheadv2_t_kernel(tc, hidden_states, weight, logit_scale, out):
@@ -48,6 +53,7 @@ def tile_geodesiclmheadv2_t_kernel(tc, hidden_states, weight, logit_scale, out):
         keep = ctx.enter_context(tc.tile_pool(name="keep", bufs=1))
         grouped_pool = ctx.enter_context(tc.tile_pool(name="grouped", bufs=3))
         x_pool = ctx.enter_context(tc.tile_pool(name="x", bufs=X_TILES))
+        gate_pool = ctx.enter_context(tc.tile_pool(name="gate", bufs=2))
         a_pool = ctx.enter_context(tc.tile_pool(name="a", bufs=A_TILES))
         turn_pool = ctx.enter_context(tc.psum_pool(name="turn", bufs=4))
         sum_pool = ctx.enter_context(tc.psum_pool(name="sum", bufs=4))
@@ -66,9 +72,10 @@ def tile_geodesiclmheadv2_t_kernel(tc, hidden_states, weight, logit_scale, out):
         nc.vector.memset(floor_b[:], 0.5e-12)
         nc.vector.memset(half[:], 0.5)
         nc.vector.memset(minus_half[:], -0.5)
-        nc.scalar.activation(out=scratch[:], in_=one[:], func=ACT.Sqrt)
+        nc.scalar.activation(out=scratch[:], in_=one[:], func=ACT.Exp)
 
         w_rows_tile = x_pool.tile([P, 4 * BANK], F32, name="w_rows_tile", tag="x", align_bytes=64)
+        w_all = w_rows_tile[:].bitcast(BF16)
         w_raw = [w_rows_tile[:, q * K : (q + 1) * K].bitcast(BF16) for q in range(W_TILES // 2)]
         h_raw = [keep.tile([P, CHUNK * SLOT], BF16, name="h_raw%d" % c) for c in range(TILES // CHUNK)]
         scale_raw = keep.tile([P, 1], BF16, name="scale_raw")
@@ -115,17 +122,10 @@ def tile_geodesiclmheadv2_t_kernel(tc, hidden_states, weight, logit_scale, out):
             )
             nc.gpsimd.tensor_tensor(out=t_coord[:, s], in0=t_raw[:, s], in1=t_up[:, s], op=ALU.mult)
 
-        time_coordinates(0, 1)
         tau = keep.tile([P, 1], F32, name="tau")
         not_neg = keep.tile([P, 1], F32, name="not_neg")
         neg = keep.tile([P, 1], F32, name="neg")
         minus_4tau = keep.tile([P, 1], F32, name="minus_4tau")
-        nc.gpsimd.tensor_scalar(out=tau[:], in0=scale_raw[:], scalar1=0.01, scalar2=2.5, op0=ALU.max, op1=ALU.min)
-        nc.gpsimd.tensor_scalar(out=not_neg[:], in0=scale_raw[:], scalar1=0.0, scalar2=-4.0, op0=ALU.is_ge, op1=ALU.mult)
-        nc.gpsimd.tensor_scalar(out=neg[:], in0=scale_raw[:], scalar1=0.0, scalar2=-4.0, op0=ALU.is_lt, op1=ALU.mult)
-        nc.gpsimd.tensor_tensor(out=not_neg[:], in0=not_neg[:], in1=neg[:], op=ALU.add)
-        nc.gpsimd.tensor_tensor(out=minus_4tau[:], in0=tau[:], in1=not_neg[:], op=ALU.mult)
-        time_coordinates(1, TILES // CHUNK)
 
         h_codes = [keep.tile([P, GROUP * P], U32, name="h_codes%d" % g, align_bytes=64) for g in range(GROUPS)]
         h_scales = [keep.tile([P, GROUP * P], U8, name="h_scales%d" % g, align_bytes=64) for g in range(GROUPS)]
@@ -181,6 +181,10 @@ def tile_geodesiclmheadv2_t_kernel(tc, hidden_states, weight, logit_scale, out):
         sumsq = keep.tile([P, W_TILES], F32, name="sumsq")
         squares = keep.tile([P, K], BF16, name="squares")
         row_ok = keep.tile([P, W_TILES], F32, name="row_ok")
+        sum_cut = keep.tile([P, W_TILES], F32, name="sum_cut")
+        halves = keep.tile([P, W_TILES], F32, name="halves")
+        squares_v = keep.tile([P, K], F32, name="squares_v")
+        nc.gpsimd.memset(halves[:], 0.5)
         norm = keep.tile([P, W_TILES], F32, name="norm")
         e_plus = keep.tile([P, W_TILES], F32, name="e_plus")
         e_minus = keep.tile([P, W_TILES], F32, name="e_minus")
@@ -237,8 +241,8 @@ def tile_geodesiclmheadv2_t_kernel(tc, hidden_states, weight, logit_scale, out):
                         identity=ident_bf[:],
                     )
 
-        def w_copy_out(q):
-            nc.scalar.copy(
+        def w_copy_out(copy, q):
+            copy(
                 out=w_grouped[q // 2][:, (q % 2) * 2 * BANK : (q % 2 + 1) * 2 * BANK].rearrange(
                     "p (j v t) -> p j v t", j=2, t=4
                 ),
@@ -286,6 +290,12 @@ def tile_geodesiclmheadv2_t_kernel(tc, hidden_states, weight, logit_scale, out):
                     op1=ALU.subtract,
                 )
 
+        def gated_clip(u):
+            gate = gate_pool.tile([P, 1], F32, name="gate", tag="gate")
+            nc.vector.memset(gate[:], X_MIN)
+            x = x_of[u][:]
+            nc.gpsimd.tensor_scalar(out=x, in0=x, scalar1=X_MAX, scalar2=gate[:, 0:1], op0=ALU.min, op1=ALU.max)
+
         def clip(eng, u, c0=0, c1=4 * BANK):
             x = x_of[u][:, c0:c1]
             eng.tensor_scalar(out=x, in0=x, scalar1=X_MAX, scalar2=X_MIN, op0=ALU.min, op1=ALU.max)
@@ -302,6 +312,11 @@ def tile_geodesiclmheadv2_t_kernel(tc, hidden_states, weight, logit_scale, out):
 
         def add_roots(u):
             nc.vector.tensor_tensor(out=a_of[u][:], in0=a_of[u][:], in1=x_of[u][:], op=ALU.add)
+
+        def square(u):
+            nc.scalar.activation(out=a_of[u][:], in_=a_of[u][:], func=ACT.Square)
+            nc.vector.tensor_scalar(out=a_of[u][:], in0=a_of[u][:], scalar1=minus_4tau[:, 0:1], scalar2=None, op0=ALU.mult)
+            nc.sync.dma_start(out=out_flat[:, 4 * BANK * u : 4 * BANK * (u + 1)], in_=a_of[u][:])
 
         sum_of = {}
 
@@ -324,37 +339,36 @@ def tile_geodesiclmheadv2_t_kernel(tc, hidden_states, weight, logit_scale, out):
             nc.vector.scalar_tensor_tensor(out=a, in0=a, scalar=minus_4tau[:, 0:1], in1=a, op0=ALU.mult, op1=ALU.mult)
             nc.sync.dma_start(out=out_flat[:, 4 * BANK * u + c0 : 4 * BANK * u + c1], in_=a)
 
-        first_half = sanitise(0, 1)
-        for step in first_half:
-            step()
         for j in range(W_TILES):
             nc.scalar.activation(out=squares[:], in_=w_row_tile(j), func=ACT.Square, accum_out=sumsq[:, j : j + 1])
-        h_transpose(0)
+        first_half = sanitise(0, 1)
         second_half = sanitise(1, 2)
-        for q in range(2):
-            nc.vector.tensor_scalar(out=w_raw[q], in0=w_raw[q], scalar1=-FMAX, scalar2=FMAX, op0=ALU.max, op1=ALU.min)
-        second_half[0]()
-        second_half[1]()
-        nc.vector.tensor_single_scalar(out=row_ok[:], in_=sumsq[:], scalar=FMAX, op=ALU.is_le)
-        nc.vector.tensor_scalar(out=sumsq[:], in0=sumsq[:], scalar1=1.0e-30, scalar2=SUMSQ_MAX, op0=ALU.max, op1=ALU.min)
-        second_half[2]()
-        second_half[3]()
-        nc.scalar.activation(out=norm[:], in_=sumsq[:], func=ACT.Sqrt)
+        for step in first_half + second_half[:2]:
+            step()
+        h_transpose(0)
+        nc.vector.tensor_scalar(out=sum_cut[:], in0=sumsq[:], scalar1=1.0e-30, scalar2=SUMSQ_MAX, op0=ALU.max, op1=ALU.min)
+        nc.gpsimd.tensor_tensor(out=norm[:], in0=sum_cut[:], in1=halves[:], op=ALU.pow)
+        time_coordinates(0, 1)
+
+        nc.gpsimd.tensor_scalar(out=tau[:], in0=scale_raw[:], scalar1=0.01, scalar2=2.5, op0=ALU.max, op1=ALU.min)
+        nc.gpsimd.tensor_scalar(out=not_neg[:], in0=scale_raw[:], scalar1=0.0, scalar2=-4.0, op0=ALU.is_ge, op1=ALU.mult)
+        nc.gpsimd.tensor_scalar(out=neg[:], in0=scale_raw[:], scalar1=0.0, scalar2=-4.0, op0=ALU.is_lt, op1=ALU.mult)
+        nc.gpsimd.tensor_tensor(out=not_neg[:], in0=not_neg[:], in1=neg[:], op=ALU.add)
+        nc.gpsimd.tensor_tensor(out=minus_4tau[:], in0=tau[:], in1=not_neg[:], op=ALU.mult)
+        time_coordinates(1, TILES // CHUNK)
         nc.scalar.activation(out=e_plus[:], in_=norm[:], func=ACT.Exp)
         nc.scalar.activation(out=e_minus[:], in_=norm[:], func=ACT.Exp, scale=-1.0)
-        h_copy_out(0)
         nc.scalar.activation(out=scratch[:], in_=one[:], func=ACT.Sqrt)
+        nc.vector.tensor_single_scalar(out=row_ok[:], in_=sumsq[:], scalar=FMAX, op=ALU.is_le)
+        nc.vector.tensor_scalar(out=w_all, in0=w_all, scalar1=-FMAX, scalar2=FMAX, op0=ALU.max, op1=ALU.min)
         nc.vector.reciprocal(out=inverse[:], in_=norm[:])
-        for q in range(2, 4):
-            nc.vector.tensor_scalar(out=w_raw[q], in0=w_raw[q], scalar1=-FMAX, scalar2=FMAX, op0=ALU.max, op1=ALU.min)
         nc.vector.tensor_tensor(out=diff[:], in0=e_plus[:], in1=e_minus[:], op=ALU.subtract)
         nc.vector.tensor_tensor(out=total[:], in0=e_plus[:], in1=e_minus[:], op=ALU.add)
         nc.vector.scalar_tensor_tensor(out=diff[:], in0=diff[:], scalar=0.5, in1=inverse[:], op0=ALU.mult, op1=ALU.mult)
         nc.vector.scalar_tensor_tensor(out=cosh_col[:], in0=total[:], scalar=0.5, in1=row_ok[:], op0=ALU.mult, op1=ALU.mult)
         nc.vector.scalar_tensor_tensor(out=r_col[:], in0=diff[:], scalar=1.0, in1=row_ok[:], op0=ALU.max, op1=ALU.mult)
-        second_half[4]()
-        h_quantise(0)
-        for step in sanitise(2, 4):
+        ahead = second_half[2:] + sanitise(2, 4)
+        for step in ahead[:HEAD_A]:
             step()
         for h in range(2):
             for j in range(4 * h, 4 * h + 4):
@@ -362,16 +376,22 @@ def tile_geodesiclmheadv2_t_kernel(tc, hidden_states, weight, logit_scale, out):
             w_transpose(2 * h)
             w_transpose(2 * h + 1)
             spread(h)
-            w_copy_out(2 * h)
-            w_copy_out(2 * h + 1)
+            if h == 0:
+                h_copy_out(0)
+                h_quantise(0)
+            w_copy_out(nc.scalar.copy, 2 * h)
+            w_copy_out(nc.scalar.copy, 2 * h + 1)
             spread_copy(h)
             w_quantise(h)
+            if h == 0:
+                for step in ahead[HEAD_A:HEAD_B]:
+                    step()
         h_transpose(1)
         h_copy_out(1)
         h_quantise(1)
-
-        late = sanitise(4, 6) + sanitise(6, 8)
+        late = ahead[HEAD_B:] + sanitise(4, 6) + sanitise(6, 8)
         turned = 2
+        quantised = 2
 
         first = 0
         previous = []
@@ -383,50 +403,54 @@ def tile_geodesiclmheadv2_t_kernel(tc, hidden_states, weight, logit_scale, out):
             late_sums = [(u, k) for u in batch if u in LATE_SUMS for k in range(4)]
             summed = []
             for k, u in enumerate(batch):
+                if k > 0 and u - 1 not in SCALAR_CLIPS + VECTOR_CLIPS:
+                    gated_clip(u - 1)
                 make_x(u)
-                if turned < GROUPS and True:
+                if quantised < turned:
+                    h_quantise(quantised)
+                    quantised += 1
+                turning = turned < GROUPS
+                if turning:
                     h_transpose(turned)
                 if u + 1 < UNITS:
                     dot(u + 1)
                 if previous:
                     finish(previous.pop(0))
-                if u not in SCALAR_CLIPS and not late:
-                    clip(nc.vector, u)
-                for step in late[:2]:
+                for step in late[:LATE_STEPS]:
                     step()
-                if u not in SCALAR_CLIPS and late:
+                late = late[LATE_STEPS:]
+                if u in VECTOR_CLIPS:
                     clip(nc.vector, u)
-                late = late[2:]
-                if k > 1 and early:
+                if early and k > early[0][0] - batch[0] + 3 and turned == GROUPS:
                     summed.append(early.pop(0))
                     sum_on_tensor(*summed[-1])
-                if turned < GROUPS:
+                if turning:
                     h_copy_out(turned)
+                    turned += 1
                 if k > 0:
                     roots(u - 1)
-                if turned < GROUPS:
-                    h_quantise(turned)
-                    turned += 1
             while early:
                 summed.append(early.pop(0))
                 sum_on_tensor(*summed[-1])
             roots(batch[-1])
             for u in previous:
                 finish(u)
+            others = [u for u in batch if u not in EARLY_SUMS + LATE_SUMS]
             for s in summed:
                 logarithm_of_sum(*s)
-                if late_sums:
-                    summed.append(late_sums.pop(0))
-                    sum_on_tensor(*summed[-1])
-                    if late_sums == []:
-                        break
-            others = [u for u in batch if u not in EARLY_SUMS + LATE_SUMS]
+            for s in late_sums:
+                sum_on_tensor(*s)
             for u in others:
                 add_roots(u)
                 logarithm(u)
-            for u, k in summed:
-                if u in LATE_SUMS:
-                    logarithm_of_sum(u, k)
+            for s in late_sums:
+                logarithm_of_sum(*s)
             previous = [u for u in batch if u in EARLY_SUMS] + others + [u for u in batch if u in LATE_SUMS]
         for u in previous:
-            finish(u)
+            if u in LATE_SUMS:
+                for k in range(4):
+                    finish(u, k * BANK, (k + 1) * BANK)
+            elif u in SQUARED:
+                square(u)
+            else:
+                finish(u)

@@ -1,4 +1,5 @@
 from contextlib import ExitStack
+from functools import partial
 
 import concourse.mybir as mybir
 from concourse.masks import make_identity
@@ -33,7 +34,7 @@ UNITS = TILES // 2
 BATCHES = (8, 8)
 X_TILES = 8
 A_TILES = 9
-EARLY_SUMS = (8,)
+EARLY_SUMS = (0, 8)
 LATE_SUMS = (9,)
 SCALAR_CLIPS = (0,)
 VECTOR_CLIPS = (7, 15)
@@ -403,11 +404,10 @@ def tile_geodesiclmheadv2_t_kernel(tc, hidden_states, weight, logit_scale, out):
             late_sums = [(u, k) for u in batch if u in LATE_SUMS for k in range(4)]
             summed = []
             for k, u in enumerate(batch):
-                if k > 0 and u - 1 not in SCALAR_CLIPS + VECTOR_CLIPS:
-                    gated_clip(u - 1)
                 make_x(u)
+                steps = []
                 if quantised < turned:
-                    h_quantise(quantised)
+                    steps.append(partial(h_quantise, quantised))
                     quantised += 1
                 turning = turned < GROUPS
                 if turning:
@@ -415,12 +415,17 @@ def tile_geodesiclmheadv2_t_kernel(tc, hidden_states, weight, logit_scale, out):
                 if u + 1 < UNITS:
                     dot(u + 1)
                 if previous:
-                    finish(previous.pop(0))
-                for step in late[:LATE_STEPS]:
-                    step()
+                    steps.append(partial(finish, previous.pop(0)))
+                steps.extend(late[:LATE_STEPS])
                 late = late[LATE_STEPS:]
                 if u in VECTOR_CLIPS:
-                    clip(nc.vector, u)
+                    steps.append(partial(clip, nc.vector, u))
+                for step in steps[:-1]:
+                    step()
+                if u not in SCALAR_CLIPS + VECTOR_CLIPS:
+                    gated_clip(u)
+                if steps:
+                    steps[-1]()
                 if early and k > early[0][0] - batch[0] + 3 and turned == GROUPS:
                     summed.append(early.pop(0))
                     sum_on_tensor(*summed[-1])

@@ -108,25 +108,29 @@ def tile_geodesiclmheadv2_t_kernel(tc, hidden_states, weight, logit_scale, out):
         t_up = keep.tile([P, TILES], F32, name="t_up")
         t_down = keep.tile([P, TILES], F32, name="t_down")
         t_coord = keep.tile([P, TILES], F32, name="t_coord")
+        tau = keep.tile([P, 1], F32, name="tau")
+        is_number = keep.tile([P, 1], F32, name="is_number")
+        minus_4tau = keep.tile([P, 1], F32, name="minus_4tau")
 
-        def time_coordinates(c0, c1):
-            for c in range(c0, c1):
-                nc.gpsimd.tensor_copy(
+        def gather_times():
+            for c in range(TILES // CHUNK):
+                nc.scalar.copy(
                     out=t_raw[:, CHUNK * c : CHUNK * (c + 1)].unsqueeze(2),
                     in_=h_raw[c][:].rearrange("p (i c) -> p i c", c=SLOT)[:, :, 1:2],
                 )
-            s = slice(CHUNK * c0, CHUNK * c1)
-            nan_to_num_factor(nc.gpsimd, t_up[:, s], t_down[:, s], t_raw[:, s])
-            nc.gpsimd.tensor_tensor(out=t_up[:, s], in0=t_up[:, s], in1=t_down[:, s], op=ALU.mult)
-            nc.gpsimd.tensor_scalar(
-                out=t_raw[:, s], in0=t_raw[:, s], scalar1=-FMAX, scalar2=FMAX, op0=ALU.max, op1=ALU.min
-            )
-            nc.gpsimd.tensor_tensor(out=t_coord[:, s], in0=t_raw[:, s], in1=t_up[:, s], op=ALU.mult)
 
-        tau = keep.tile([P, 1], F32, name="tau")
-        not_neg = keep.tile([P, 1], F32, name="not_neg")
-        neg = keep.tile([P, 1], F32, name="neg")
-        minus_4tau = keep.tile([P, 1], F32, name="minus_4tau")
+        def time_coordinates():
+            nan_to_num_factor(nc.vector, t_up[:], t_down[:], t_raw[:])
+            nc.vector.tensor_scalar(out=t_raw[:], in0=t_raw[:], scalar1=-FMAX, scalar2=FMAX, op0=ALU.max, op1=ALU.min)
+            nc.vector.tensor_tensor(out=t_up[:], in0=t_up[:], in1=t_down[:], op=ALU.mult)
+            nc.vector.tensor_tensor(out=t_coord[:], in0=t_raw[:], in1=t_up[:], op=ALU.mult)
+
+        def temperature():
+            nc.vector.tensor_scalar(out=tau[:], in0=scale_raw[:], scalar1=0.01, scalar2=2.5, op0=ALU.max, op1=ALU.min)
+            nc.vector.tensor_tensor(out=is_number[:], in0=scale_raw[:], in1=scale_raw[:], op=ALU.is_equal)
+            nc.vector.scalar_tensor_tensor(
+                out=minus_4tau[:], in0=tau[:], scalar=-4.0, in1=is_number[:], op0=ALU.mult, op1=ALU.mult
+            )
 
         h_codes = [keep.tile([P, GROUP * P], U32, name="h_codes%d" % g, align_bytes=64) for g in range(GROUPS)]
         h_scales = [keep.tile([P, GROUP * P], U8, name="h_scales%d" % g, align_bytes=64) for g in range(GROUPS)]
@@ -349,14 +353,6 @@ def tile_geodesiclmheadv2_t_kernel(tc, hidden_states, weight, logit_scale, out):
         h_transpose(0)
         nc.vector.tensor_scalar(out=sum_cut[:], in0=sumsq[:], scalar1=1.0e-30, scalar2=SUMSQ_MAX, op0=ALU.max, op1=ALU.min)
         nc.gpsimd.tensor_tensor(out=norm[:], in0=sum_cut[:], in1=halves[:], op=ALU.pow)
-        time_coordinates(0, 1)
-
-        nc.gpsimd.tensor_scalar(out=tau[:], in0=scale_raw[:], scalar1=0.01, scalar2=2.5, op0=ALU.max, op1=ALU.min)
-        nc.gpsimd.tensor_scalar(out=not_neg[:], in0=scale_raw[:], scalar1=0.0, scalar2=-4.0, op0=ALU.is_ge, op1=ALU.mult)
-        nc.gpsimd.tensor_scalar(out=neg[:], in0=scale_raw[:], scalar1=0.0, scalar2=-4.0, op0=ALU.is_lt, op1=ALU.mult)
-        nc.gpsimd.tensor_tensor(out=not_neg[:], in0=not_neg[:], in1=neg[:], op=ALU.add)
-        nc.gpsimd.tensor_tensor(out=minus_4tau[:], in0=tau[:], in1=not_neg[:], op=ALU.mult)
-        time_coordinates(1, TILES // CHUNK)
         nc.scalar.activation(out=e_plus[:], in_=norm[:], func=ACT.Exp)
         nc.scalar.activation(out=e_minus[:], in_=norm[:], func=ACT.Exp, scale=-1.0)
         nc.scalar.activation(out=scratch[:], in_=one[:], func=ACT.Sqrt)
@@ -385,8 +381,11 @@ def tile_geodesiclmheadv2_t_kernel(tc, hidden_states, weight, logit_scale, out):
             spread_copy(h)
             w_quantise(h)
             if h == 0:
+                gather_times()
                 for step in ahead[HEAD_A:HEAD_B]:
                     step()
+                temperature()
+                time_coordinates()
         h_transpose(1)
         h_copy_out(1)
         h_quantise(1)

@@ -52,7 +52,7 @@ def tile_geodesiclmheadv2_t_kernel(tc, hidden_states, weight, logit_scale, out):
 
     with ExitStack() as ctx:
         keep = ctx.enter_context(tc.tile_pool(name="keep", bufs=1))
-        grouped_pool = ctx.enter_context(tc.tile_pool(name="grouped", bufs=3))
+        grouped_pool = ctx.enter_context(tc.tile_pool(name="grouped", bufs=5))
         x_pool = ctx.enter_context(tc.tile_pool(name="x", bufs=X_TILES))
         gate_pool = ctx.enter_context(tc.tile_pool(name="gate", bufs=2))
         a_pool = ctx.enter_context(tc.tile_pool(name="a", bufs=A_TILES))
@@ -389,7 +389,10 @@ def tile_geodesiclmheadv2_t_kernel(tc, hidden_states, weight, logit_scale, out):
         h_transpose(1)
         h_copy_out(1)
         h_quantise(1)
-        late = ahead[HEAD_B:] + sanitise(4, 6) + sanitise(6, 8)
+        late = [(step, 4) for step in ahead[HEAD_B:]]
+        for c in range(2, TILES // CHUNK):
+            late.extend(zip(sanitise(2 * c, 2 * c + 2), (2 * c, 2 * c, 2 * c, 2 * c, 2 * c + 2)))
+        ready = 4
         turned = 2
         quantised = 2
 
@@ -405,18 +408,20 @@ def tile_geodesiclmheadv2_t_kernel(tc, hidden_states, weight, logit_scale, out):
             for k, u in enumerate(batch):
                 make_x(u)
                 steps = []
-                if quantised < turned:
+                if quantised < turned and 2 * quantised <= u + 3:
                     steps.append(partial(h_quantise, quantised))
                     quantised += 1
-                turning = turned < GROUPS
+                turning = turned < ready
                 if turning:
                     h_transpose(turned)
                 if u + 1 < UNITS:
                     dot(u + 1)
                 if previous:
                     steps.append(partial(finish, previous.pop(0)))
-                steps.extend(late[:LATE_STEPS])
-                late = late[LATE_STEPS:]
+                for n in range(2 - u % 2):
+                    if late:
+                        step, ready = late.pop(0)
+                        steps.append(step)
                 if u in VECTOR_CLIPS:
                     steps.append(partial(clip, nc.vector, u))
                 for step in steps[:-1]:
@@ -431,14 +436,18 @@ def tile_geodesiclmheadv2_t_kernel(tc, hidden_states, weight, logit_scale, out):
                 if turning:
                     h_copy_out(turned)
                     turned += 1
-                if k > 0:
+                if k > 0 and u - 1 not in SCALAR_CLIPS:
                     roots(u - 1)
+                if u in SCALAR_CLIPS:
+                    roots(u)
             while early:
                 summed.append(early.pop(0))
                 sum_on_tensor(*summed[-1])
-            roots(batch[-1])
+            if batch[-1] not in SCALAR_CLIPS:
+                roots(batch[-1])
             for u in previous:
                 finish(u)
+            pieces = ((0, 4 * BANK),) if first < UNITS else ((0, 2 * BANK), (2 * BANK, 4 * BANK))
             others = [u for u in batch if u not in EARLY_SUMS + LATE_SUMS]
             for s in summed:
                 logarithm_of_sum(*s)
@@ -446,15 +455,15 @@ def tile_geodesiclmheadv2_t_kernel(tc, hidden_states, weight, logit_scale, out):
                 sum_on_tensor(*s)
             for u in others:
                 add_roots(u)
-                logarithm(u)
+                for c0, c1 in pieces:
+                    logarithm(u, c0, c1)
             for s in late_sums:
                 logarithm_of_sum(*s)
             previous = [u for u in batch if u in EARLY_SUMS] + others + [u for u in batch if u in LATE_SUMS]
         for u in previous:
-            if u in LATE_SUMS:
+            if u in EARLY_SUMS + LATE_SUMS:
                 for k in range(4):
                     finish(u, k * BANK, (k + 1) * BANK)
-            elif u in SQUARED:
-                square(u)
             else:
-                finish(u)
+                for c0, c1 in pieces:
+                    finish(u, c0, c1)

@@ -31,23 +31,21 @@ X_MAX = 3.4028234663852886e38
 FLOPS = 2 * TOKENS * VOCAB * K
 
 UNITS = TILES // 2
-BATCHES = (8, 8)
 X_TILES = 8
 A_TILES = 9
+MIDDLE = 10
+BATCHES = (8, 8)
 EARLY_SUMS = (0, 8)
-LATE_SUMS = (9,)
+LATE_SUMS = ()
 SCALAR_CLIPS = (0,)
 VECTOR_CLIPS = (7, 15)
-SQUARED = ()
-HEAD_A = 8
-HEAD_B = 8
-LATE_STEPS = 2
 
 
 def tile_geodesiclmheadv2_t_kernel(tc, hidden_states, weight, logit_scale, out):
     nc = tc.nc
     hid = hidden_states.flatten_outer_dims().rearrange("(p i) c -> p i c", i=TILES)
     out_flat = out.flatten_outer_dims().rearrange("(p i) v -> p (i v)", i=TILES)
+    out_tiles = out.flatten_outer_dims().rearrange("(p i) v -> p i v", i=TILES)
     w_rows = weight.rearrange("(j p) k -> p j k", p=P)
 
     with ExitStack() as ctx:
@@ -108,6 +106,8 @@ def tile_geodesiclmheadv2_t_kernel(tc, hidden_states, weight, logit_scale, out):
         t_up = keep.tile([P, TILES], F32, name="t_up")
         t_down = keep.tile([P, TILES], F32, name="t_down")
         t_coord = keep.tile([P, TILES], F32, name="t_coord")
+        t_row = keep.tile([P, (GROUPS - MIDDLE // 2) * BANK], F32, name="t_row")
+        t_turned = {}
         tau = keep.tile([P, 1], F32, name="tau")
         is_number = keep.tile([P, 1], F32, name="is_number")
         minus_4tau = keep.tile([P, 1], F32, name="minus_4tau")
@@ -120,17 +120,37 @@ def tile_geodesiclmheadv2_t_kernel(tc, hidden_states, weight, logit_scale, out):
                 )
 
         def time_coordinates():
-            nan_to_num_factor(nc.vector, t_up[:], t_down[:], t_raw[:])
-            nc.vector.tensor_scalar(out=t_raw[:], in0=t_raw[:], scalar1=-FMAX, scalar2=FMAX, op0=ALU.max, op1=ALU.min)
-            nc.vector.tensor_tensor(out=t_up[:], in0=t_up[:], in1=t_down[:], op=ALU.mult)
-            nc.vector.tensor_tensor(out=t_coord[:], in0=t_raw[:], in1=t_up[:], op=ALU.mult)
+            return [
+                lambda: nc.vector.tensor_scalar(out=t_up[:], in0=t_raw[:], scalar1=FMAX, scalar2=C_INF, op0=ALU.is_le, op1=ALU.add),
+                lambda: nc.vector.tensor_scalar(out=t_down[:], in0=t_raw[:], scalar1=-FMAX, scalar2=C_INF, op0=ALU.is_ge, op1=ALU.add),
+                lambda: nc.vector.tensor_scalar(out=t_raw[:], in0=t_raw[:], scalar1=-FMAX, scalar2=FMAX, op0=ALU.max, op1=ALU.min),
+                lambda: nc.vector.tensor_tensor(out=t_up[:], in0=t_up[:], in1=t_down[:], op=ALU.mult),
+                lambda: nc.vector.tensor_tensor(out=t_coord[:], in0=t_raw[:], in1=t_up[:], op=ALU.mult),
+            ]
+
+        def spread_times(g):
+            bank = turn_pool.tile([P, BANK], F32, name="t_turned", tag="turn")
+            t_turned[g] = bank
+            for ii in range(GROUP):
+                i = GROUP * g + ii
+                nc.tensor.transpose(
+                    out=bank[:, ii * P : (ii + 1) * P],
+                    in_=t_coord[:, i : i + 1].to_broadcast([P, P]),
+                    identity=ident[:],
+                )
+
+        def copy_times(g):
+            g0 = g - MIDDLE // 2
+            nc.vector.tensor_copy(out=t_row[:, g0 * BANK : (g0 + 1) * BANK], in_=t_turned[g][:])
 
         def temperature():
-            nc.vector.tensor_scalar(out=tau[:], in0=scale_raw[:], scalar1=0.01, scalar2=2.5, op0=ALU.max, op1=ALU.min)
-            nc.vector.tensor_tensor(out=is_number[:], in0=scale_raw[:], in1=scale_raw[:], op=ALU.is_equal)
-            nc.vector.scalar_tensor_tensor(
-                out=minus_4tau[:], in0=tau[:], scalar=-4.0, in1=is_number[:], op0=ALU.mult, op1=ALU.mult
-            )
+            return [
+                lambda: nc.vector.tensor_scalar(out=tau[:], in0=scale_raw[:], scalar1=0.01, scalar2=2.5, op0=ALU.max, op1=ALU.min),
+                lambda: nc.vector.tensor_tensor(out=is_number[:], in0=scale_raw[:], in1=scale_raw[:], op=ALU.is_equal),
+                lambda: nc.vector.scalar_tensor_tensor(
+                    out=minus_4tau[:], in0=tau[:], scalar=-4.0, in1=is_number[:], op0=ALU.mult, op1=ALU.mult
+                ),
+            ]
 
         h_codes = [keep.tile([P, GROUP * P], U32, name="h_codes%d" % g, align_bytes=64) for g in range(GROUPS)]
         h_scales = [keep.tile([P, GROUP * P], U8, name="h_scales%d" % g, align_bytes=64) for g in range(GROUPS)]
@@ -145,7 +165,8 @@ def tile_geodesiclmheadv2_t_kernel(tc, hidden_states, weight, logit_scale, out):
             n = (g1 - g0) * GROUP
             first = (g0 % 2) * GROUP
             x = h_raw[g0 // 2][:].rearrange("p (i c) -> p i c", c=SLOT)[:, first : first + n, 2 : K + 2]
-            up, down = factor_up[:, 0 : n * K], factor_down[:, 0 : n * K]
+            c0 = first * K if n == GROUP else 0
+            up, down = factor_up[:, c0 : c0 + n * K], factor_down[:, c0 : c0 + n * K]
             up3 = up.rearrange("p (i c) -> p i c", c=K)
             down3 = down.rearrange("p (i c) -> p i c", c=K)
             return [
@@ -267,11 +288,23 @@ def tile_geodesiclmheadv2_t_kernel(tc, hidden_states, weight, logit_scale, out):
 
         def dot(u):
             for k in range(4):
+                bank = sum_pool.tile([P, BANK], F32, name="dot", tag="sum")
+                dot_of[(u, k)] = bank
+                if u >= MIDDLE:
+                    g, j = u // 2, 4 * (u % 2) + k
+                    nc.tensor.matmul_mx(
+                        out=bank[:],
+                        lhsT=w_codes[:, j * P : (j + 1) * P].bitcast(FP8X4),
+                        lhsT_scale=w_scales[:, j * P : (j + 1) * P],
+                        rhs=h_codes[g][:].bitcast(FP8X4),
+                        rhs_scale=h_scales[g][:],
+                        start=True,
+                        stop=True,
+                    )
+                    continue
                 i, h = 2 * u + k // 2, k % 2
                 g = i // GROUP
                 tokens = slice((i % GROUP) * P, (i % GROUP + 1) * P)
-                bank = sum_pool.tile([P, BANK], F32, name="dot", tag="sum")
-                dot_of[(u, k)] = bank
                 nc.tensor.matmul_mx(
                     out=bank[:],
                     lhsT=h_codes[g][:, tokens].bitcast(FP8X4),
@@ -284,7 +317,19 @@ def tile_geodesiclmheadv2_t_kernel(tc, hidden_states, weight, logit_scale, out):
 
         def make_x(u):
             x_of[u] = x_pool.tile([P, 4 * BANK], F32, name="x", tag="x", align_bytes=64)
+            x4 = x_of[u][:].rearrange("p (i j c) -> p j i c", i=4, j=4)
             for k in range(4):
+                if u >= MIDDLE:
+                    g, j = u // 2 - MIDDLE // 2, 4 * (u % 2) + k
+                    nc.vector.scalar_tensor_tensor(
+                        out=x4[:, k, :, :],
+                        in0=t_row[:, g * BANK : (g + 1) * BANK].rearrange("p (i c) -> p i c", i=4),
+                        scalar=cosh_col[:, j : j + 1],
+                        in1=dot_of[(u, k)][:].rearrange("p (i c) -> p i c", i=4),
+                        op0=ALU.mult,
+                        op1=ALU.subtract,
+                    )
+                    continue
                 i, h = 2 * u + k // 2, k % 2
                 nc.vector.scalar_tensor_tensor(
                     out=x_of[u][:, k * BANK : (k + 1) * BANK],
@@ -336,6 +381,30 @@ def tile_geodesiclmheadv2_t_kernel(tc, hidden_states, weight, logit_scale, out):
             c = slice(k * BANK, (k + 1) * BANK)
             nc.scalar.activation(out=a_of[u][:, c], in_=sum_of[(u, k)][:], func=ACT.Ln)
 
+        def turn_and_add(u, ii):
+            bank = turn_pool.tile([P, BANK], F32, name="root_sum", tag="turn")
+            sum_of[(u, ii)] = bank
+            for jj in range(4):
+                c = slice((4 * ii + jj) * P, (4 * ii + jj + 1) * P)
+                for part in (a_of[u], x_of[u]):
+                    nc.tensor.matmul(
+                        out=bank[:, jj * P : (jj + 1) * P],
+                        lhsT=part[:, c],
+                        rhs=ident[:],
+                        start=part is a_of[u],
+                        stop=part is x_of[u],
+                        is_transpose=True,
+                    )
+
+        def finish_turned(u, i0, i1):
+            a = a_of[u][:, i0 * BANK : i1 * BANK]
+            nc.vector.scalar_tensor_tensor(out=a, in0=a, scalar=minus_4tau[:, 0:1], in1=a, op0=ALU.mult, op1=ALU.mult)
+            g, h = u // 2, u % 2
+            nc.sync.dma_start(
+                out=out_tiles[:, GROUP * g + i0 : GROUP * g + i1, h * BANK : (h + 1) * BANK],
+                in_=a.rearrange("p (i v) -> p i v", v=BANK),
+            )
+
         def logarithm(u, c0=0, c1=4 * BANK):
             nc.scalar.activation(out=a_of[u][:, c0:c1], in_=a_of[u][:, c0:c1], func=ACT.Ln)
 
@@ -348,7 +417,7 @@ def tile_geodesiclmheadv2_t_kernel(tc, hidden_states, weight, logit_scale, out):
             nc.scalar.activation(out=squares[:], in_=w_row_tile(j), func=ACT.Square, accum_out=sumsq[:, j : j + 1])
         first_half = sanitise(0, 1)
         second_half = sanitise(1, 2)
-        for step in first_half + second_half[:2]:
+        for step in first_half[:4] + second_half[:1] + first_half[4:] + second_half[1:2]:
             step()
         h_transpose(0)
         nc.vector.tensor_scalar(out=sum_cut[:], in0=sumsq[:], scalar1=1.0e-30, scalar2=SUMSQ_MAX, op0=ALU.max, op1=ALU.min)
@@ -364,8 +433,8 @@ def tile_geodesiclmheadv2_t_kernel(tc, hidden_states, weight, logit_scale, out):
         nc.vector.scalar_tensor_tensor(out=diff[:], in0=diff[:], scalar=0.5, in1=inverse[:], op0=ALU.mult, op1=ALU.mult)
         nc.vector.scalar_tensor_tensor(out=cosh_col[:], in0=total[:], scalar=0.5, in1=row_ok[:], op0=ALU.mult, op1=ALU.mult)
         nc.vector.scalar_tensor_tensor(out=r_col[:], in0=diff[:], scalar=1.0, in1=row_ok[:], op0=ALU.max, op1=ALU.mult)
-        ahead = second_half[2:] + sanitise(2, 4)
-        for step in ahead[:HEAD_A]:
+        ahead = sanitise(2, 4)
+        for step in second_half[2:4] + ahead[:1] + second_half[4:]:
             step()
         for h in range(2):
             for j in range(4 * h, 4 * h + 4):
@@ -375,21 +444,29 @@ def tile_geodesiclmheadv2_t_kernel(tc, hidden_states, weight, logit_scale, out):
             spread(h)
             if h == 0:
                 h_copy_out(0)
+                for step, short in zip(ahead[1:4], temperature()):
+                    step()
+                    short()
                 h_quantise(0)
             w_copy_out(nc.scalar.copy, 2 * h)
             w_copy_out(nc.scalar.copy, 2 * h + 1)
             spread_copy(h)
-            w_quantise(h)
             if h == 0:
                 gather_times()
-                for step in ahead[HEAD_A:HEAD_B]:
-                    step()
-                temperature()
-                time_coordinates()
+                times = time_coordinates()
+                times[0]()
+                times[1]()
+                w_quantise(0)
+                times[2]()
+                times[3]()
+                ahead[4]()
+                times[4]()
+            else:
+                w_quantise(1)
         h_transpose(1)
         h_copy_out(1)
         h_quantise(1)
-        late = [(step, 4) for step in ahead[HEAD_B:]]
+        late = []
         for c in range(2, TILES // CHUNK):
             late.extend(zip(sanitise(2 * c, 2 * c + 2), (2 * c, 2 * c, 2 * c, 2 * c, 2 * c + 2)))
         ready = 4
@@ -418,12 +495,16 @@ def tile_geodesiclmheadv2_t_kernel(tc, hidden_states, weight, logit_scale, out):
                     dot(u + 1)
                 if previous:
                     steps.append(partial(finish, previous.pop(0)))
-                for n in range(2 - u % 2):
+                for n in range(1 + u % 2):
                     if late:
                         step, ready = late.pop(0)
                         steps.append(step)
                 if u in VECTOR_CLIPS:
                     steps.append(partial(clip, nc.vector, u))
+                if 8 <= u < 8 + GROUPS - MIDDLE // 2:
+                    spread_times(MIDDLE // 2 + u - 8)
+                if 8 < u <= 8 + GROUPS - MIDDLE // 2:
+                    steps.insert(0, partial(copy_times, MIDDLE // 2 + u - 1 - 8))
                 for step in steps[:-1]:
                     step()
                 if u not in SCALAR_CLIPS + VECTOR_CLIPS:
@@ -448,7 +529,8 @@ def tile_geodesiclmheadv2_t_kernel(tc, hidden_states, weight, logit_scale, out):
             for u in previous:
                 finish(u)
             pieces = ((0, 4 * BANK),) if first < UNITS else ((0, 2 * BANK), (2 * BANK, 4 * BANK))
-            others = [u for u in batch if u not in EARLY_SUMS + LATE_SUMS]
+            others = [u for u in batch if u not in EARLY_SUMS + LATE_SUMS and u < MIDDLE]
+            turned_units = [u for u in batch if u >= MIDDLE]
             for s in summed:
                 logarithm_of_sum(*s)
             for s in late_sums:
@@ -457,11 +539,18 @@ def tile_geodesiclmheadv2_t_kernel(tc, hidden_states, weight, logit_scale, out):
                 add_roots(u)
                 for c0, c1 in pieces:
                     logarithm(u, c0, c1)
+            for u in turned_units:
+                for ii in range(4):
+                    turn_and_add(u, ii)
+                    logarithm_of_sum(u, ii)
             for s in late_sums:
                 logarithm_of_sum(*s)
-            previous = [u for u in batch if u in EARLY_SUMS] + others + [u for u in batch if u in LATE_SUMS]
+            previous = [u for u in batch if u in EARLY_SUMS] + others + turned_units + [u for u in batch if u in LATE_SUMS]
         for u in previous:
-            if u in EARLY_SUMS + LATE_SUMS:
+            if u >= MIDDLE:
+                for ii in range(4):
+                    finish_turned(u, ii, ii + 1)
+            elif u in EARLY_SUMS + LATE_SUMS:
                 for k in range(4):
                     finish(u, k * BANK, (k + 1) * BANK)
             else:

@@ -33,7 +33,7 @@ FLOPS = 2 * TOKENS * VOCAB * K
 UNITS = TILES // 2
 X_TILES = 8
 A_TILES = 9
-MIDDLE = 10
+MIDDLE = 12
 BATCHES = (8, 8)
 EARLY_SUMS = (0, 8)
 LATE_SUMS = ()
@@ -86,11 +86,12 @@ def tile_geodesiclmheadv2_t_kernel(tc, hidden_states, weight, logit_scale, out):
                 in_=hid[:, i0:i1, :],
             )
 
-        h_load(0, GROUP)
         for q in range(W_TILES // 2):
             nc.sync.dma_start(
                 out=w_raw[q].rearrange("p (j k) -> p j k", k=K), in_=w_rows[:, 2 * q : 2 * q + 2, :]
             )
+            if q == 0:
+                h_load(0, GROUP)
         h_load(GROUP, CHUNK)
         nc.sync.dma_start(out=scale_raw[:], in_=logit_scale.partition_broadcast(P))
         for c in range(1, TILES // CHUNK):
@@ -193,10 +194,11 @@ def tile_geodesiclmheadv2_t_kernel(tc, hidden_states, weight, logit_scale, out):
                         )
 
         def h_copy_out(g):
+            copy = nc.vector.tensor_copy if g >= 6 else nc.scalar.copy
             grouped_of[g] = grouped_pool.tile([P, GROUP * K], BF16, name="grouped", tag="grouped", align_bytes=64)
             words = grouped_of[g][:].bitcast(F32).rearrange("p (t u) -> p t u", u=2)
             for pair in range(2):
-                nc.scalar.copy(
+                copy(
                     out=words[:, pair * 2 * P : (pair + 1) * 2 * P, :],
                     in_=turned_of[(g, pair)][:].rearrange("p (u t) -> p t u", u=2),
                 )
@@ -465,13 +467,12 @@ def tile_geodesiclmheadv2_t_kernel(tc, hidden_states, weight, logit_scale, out):
                 w_quantise(1)
         h_transpose(1)
         h_copy_out(1)
-        h_quantise(1)
         late = []
         for c in range(2, TILES // CHUNK):
             late.extend(zip(sanitise(2 * c, 2 * c + 2), (2 * c, 2 * c, 2 * c, 2 * c, 2 * c + 2)))
         ready = 4
         turned = 2
-        quantised = 2
+        quantised = 1
 
         first = 0
         previous = []
@@ -488,7 +489,7 @@ def tile_geodesiclmheadv2_t_kernel(tc, hidden_states, weight, logit_scale, out):
                 if quantised < turned and 2 * quantised <= u + 3:
                     steps.append(partial(h_quantise, quantised))
                     quantised += 1
-                turning = turned < ready
+                turning = turned < ready and (turned < 6 or u >= 8)
                 if turning:
                     h_transpose(turned)
                 if u + 1 < UNITS:
@@ -511,7 +512,7 @@ def tile_geodesiclmheadv2_t_kernel(tc, hidden_states, weight, logit_scale, out):
                     gated_clip(u)
                 if steps:
                     steps[-1]()
-                if early and k > early[0][0] - batch[0] + 3 and turned == GROUPS:
+                if early and k > early[0][0] - batch[0] + 3 and turned >= 6:
                     summed.append(early.pop(0))
                     sum_on_tensor(*summed[-1])
                 if turning:
@@ -537,15 +538,20 @@ def tile_geodesiclmheadv2_t_kernel(tc, hidden_states, weight, logit_scale, out):
                 sum_on_tensor(*s)
             for u in others:
                 add_roots(u)
-                for c0, c1 in pieces:
-                    logarithm(u, c0, c1)
-            for u in turned_units:
-                for ii in range(4):
-                    turn_and_add(u, ii)
-                    logarithm_of_sum(u, ii)
+            tail = []
+            for n in range(max(len(others), len(turned_units))):
+                tail.extend(others[n : n + 1] + turned_units[n : n + 1])
+            for u in tail:
+                if u < MIDDLE:
+                    for c0, c1 in pieces:
+                        logarithm(u, c0, c1)
+                else:
+                    for ii in range(4):
+                        turn_and_add(u, ii)
+                        logarithm_of_sum(u, ii)
             for s in late_sums:
                 logarithm_of_sum(*s)
-            previous = [u for u in batch if u in EARLY_SUMS] + others + turned_units + [u for u in batch if u in LATE_SUMS]
+            previous = [u for u in batch if u in EARLY_SUMS] + tail + [u for u in batch if u in LATE_SUMS]
         for u in previous:
             if u >= MIDDLE:
                 for ii in range(4):

@@ -426,7 +426,6 @@ def tile_geodesiclmheadv2_t_kernel(tc, hidden_states, weight, logit_scale, out):
         nc.gpsimd.tensor_tensor(out=norm[:], in0=sum_cut[:], in1=halves[:], op=ALU.pow)
         nc.scalar.activation(out=e_plus[:], in_=norm[:], func=ACT.Exp)
         nc.scalar.activation(out=e_minus[:], in_=norm[:], func=ACT.Exp, scale=-1.0)
-        nc.scalar.activation(out=scratch[:], in_=one[:], func=ACT.Sqrt)
         nc.vector.tensor_single_scalar(out=row_ok[:], in_=sumsq[:], scalar=FMAX, op=ALU.is_le)
         nc.vector.tensor_scalar(out=w_all, in0=w_all, scalar1=-FMAX, scalar2=FMAX, op0=ALU.max, op1=ALU.min)
         nc.vector.reciprocal(out=inverse[:], in_=norm[:])
@@ -461,16 +460,16 @@ def tile_geodesiclmheadv2_t_kernel(tc, hidden_states, weight, logit_scale, out):
                 w_quantise(0)
                 times[2]()
                 times[3]()
-                ahead[4]()
                 times[4]()
             else:
                 w_quantise(1)
         h_transpose(1)
         h_copy_out(1)
-        late = []
+        nc.scalar.activation(out=scratch[:], in_=one[:], func=ACT.Sqrt)
+        late = [(ahead[4], 4)]
         for c in range(2, TILES // CHUNK):
             late.extend(zip(sanitise(2 * c, 2 * c + 2), (2 * c, 2 * c, 2 * c, 2 * c, 2 * c + 2)))
-        ready = 4
+        ready = 2
         turned = 2
         quantised = 1
 
@@ -496,7 +495,7 @@ def tile_geodesiclmheadv2_t_kernel(tc, hidden_states, weight, logit_scale, out):
                     dot(u + 1)
                 if previous:
                     steps.append(partial(finish, previous.pop(0)))
-                for n in range(1 + u % 2):
+                for n in range(2 if u % 3 == 1 else 1):
                     if late:
                         step, ready = late.pop(0)
                         steps.append(step)
@@ -554,8 +553,9 @@ def tile_geodesiclmheadv2_t_kernel(tc, hidden_states, weight, logit_scale, out):
             previous = [u for u in batch if u in EARLY_SUMS] + tail + [u for u in batch if u in LATE_SUMS]
         for u in previous:
             if u >= MIDDLE:
-                for ii in range(4):
-                    finish_turned(u, ii, ii + 1)
+                n = 1 if u == UNITS - 1 else 2
+                for ii in range(0, 4, n):
+                    finish_turned(u, ii, ii + n)
             elif u in EARLY_SUMS + LATE_SUMS:
                 for k in range(4):
                     finish(u, k * BANK, (k + 1) * BANK)

from contextlib import ExitStack
from functools import partial

import concourse.mybir as mybir
from concourse.masks import make_identity

F32 = mybir.dt.float32
BF16 = mybir.dt.bfloat16
U32 = mybir.dt.uint32
U8 = mybir.dt.uint8
FP8X4 = mybir.dt.float8_e4m3fn_x4
ALU = mybir.AluOpType
ACT = mybir.ActivationFunctionType

P = 128
TOKENS = 4096
VOCAB = 1024
K = 512
BANK = 512
TILES = TOKENS // P
CHUNK = 8
GROUP = 4
GROUPS = TILES // GROUP
W_TILES = VOCAB // P
SLOT = 528
FMAX = 3.3895313892515355e38
C_INF = 1.0e4 / FMAX
SUMSQ_MAX = 7.0e3
X_MIN = 1.0 + 2.0**-23
X_MAX = 3.4028234663852886e38
FLOPS = 2 * TOKENS * VOCAB * K

UNITS = TILES // 2
X_TILES = 8
A_TILES = 9
MIDDLE = 12
BATCHES = (8, 8)
EARLY_SUMS = (0, 8)
LATE_SUMS = ()
SCALAR_CLIPS = (0,)
VECTOR_CLIPS = (7, 15)


def tile_geodesiclmheadv2_t_kernel(tc, hidden_states, weight, logit_scale, out):
    nc = tc.nc
    hid = hidden_states.flatten_outer_dims().rearrange("(p i) c -> p i c", i=TILES)
    out_flat = out.flatten_outer_dims().rearrange("(p i) v -> p (i v)", i=TILES)
    out_tiles = out.flatten_outer_dims().rearrange("(p i) v -> p i v", i=TILES)
    w_rows = weight.rearrange("(j p) k -> p j k", p=P)

    with ExitStack() as ctx:
        keep = ctx.enter_context(tc.tile_pool(name="keep", bufs=1))
        grouped_pool = ctx.enter_context(tc.tile_pool(name="grouped", bufs=5))
        x_pool = ctx.enter_context(tc.tile_pool(name="x", bufs=X_TILES))
        gate_pool = ctx.enter_context(tc.tile_pool(name="gate", bufs=2))
        a_pool = ctx.enter_context(tc.tile_pool(name="a", bufs=A_TILES))
        turn_pool = ctx.enter_context(tc.psum_pool(name="turn", bufs=4))
        sum_pool = ctx.enter_context(tc.psum_pool(name="sum", bufs=4))
        ctx.enter_context(tc.manual_schedule())

        ident = keep.tile([P, P], F32, name="ident")
        one = keep.tile([P, 1], F32, name="one")
        half = keep.tile([P, 1], F32, name="half")
        minus_half = keep.tile([P, 1], F32, name="minus_half")
        scratch = keep.tile([P, 1], F32, name="scratch")
        ident_bf = keep.tile([P, P], BF16, name="ident_bf")
        nc.vector.memset(one[:], 1.0)
        minus_one = keep.tile([P, 1], F32, name="minus_one")
        floor_b = keep.tile([P, 1], F32, name="floor_b")
        nc.vector.memset(minus_one[:], -1.0)
        nc.vector.memset(floor_b[:], 0.5e-12)
        nc.vector.memset(half[:], 0.5)
        nc.vector.memset(minus_half[:], -0.5)
        nc.scalar.activation(out=scratch[:], in_=one[:], func=ACT.Exp)

        w_rows_tile = x_pool.tile([P, 4 * BANK], F32, name="w_rows_tile", tag="x", align_bytes=64)
        w_all = w_rows_tile[:].bitcast(BF16)
        w_raw = [w_rows_tile[:, q * K : (q + 1) * K].bitcast(BF16) for q in range(W_TILES // 2)]
        h_raw = [keep.tile([P, CHUNK * SLOT], BF16, name="h_raw%d" % c) for c in range(TILES // CHUNK)]
        scale_raw = keep.tile([P, 1], BF16, name="scale_raw")

        def h_load(i0, i1):
            c, first = i0 // CHUNK, i0 % CHUNK
            nc.sync.dma_start(
                out=h_raw[c][:].rearrange("p (i c) -> p i c", c=SLOT)[:, first : first + i1 - i0, 1 : K + 2],
                in_=hid[:, i0:i1, :],
            )

        for q in range(W_TILES // 2):
            nc.sync.dma_start(
                out=w_raw[q].rearrange("p (j k) -> p j k", k=K), in_=w_rows[:, 2 * q : 2 * q + 2, :]
            )
            if q == 0:
                h_load(0, GROUP)
        h_load(GROUP, CHUNK)
        nc.sync.dma_start(out=scale_raw[:], in_=logit_scale.partition_broadcast(P))
        for c in range(1, TILES // CHUNK):
            h_load(CHUNK * c, CHUNK * (c + 1))
        make_identity(nc, ident[:])
        make_identity(nc, ident_bf[:])

        def nan_to_num_factor(eng, up, down, x):
            eng.tensor_scalar(out=up, in0=x, scalar1=FMAX, scalar2=C_INF, op0=ALU.is_le, op1=ALU.add)
            eng.tensor_scalar(out=down, in0=x, scalar1=-FMAX, scalar2=C_INF, op0=ALU.is_ge, op1=ALU.add)

        t_raw = keep.tile([P, TILES], F32, name="t_raw")
        t_up = keep.tile([P, TILES], F32, name="t_up")
        t_down = keep.tile([P, TILES], F32, name="t_down")
        t_coord = keep.tile([P, TILES], F32, name="t_coord")
        t_row = keep.tile([P, (GROUPS - MIDDLE // 2) * BANK], F32, name="t_row")
        t_turned = {}
        tau = keep.tile([P, 1], F32, name="tau")
        is_number = keep.tile([P, 1], F32, name="is_number")
        minus_4tau = keep.tile([P, 1], F32, name="minus_4tau")

        def gather_times():
            for c in range(TILES // CHUNK):
                nc.scalar.copy(
                    out=t_raw[:, CHUNK * c : CHUNK * (c + 1)].unsqueeze(2),
                    in_=h_raw[c][:].rearrange("p (i c) -> p i c", c=SLOT)[:, :, 1:2],
                )

        def time_coordinates():
            return [
                lambda: nc.vector.tensor_scalar(out=t_up[:], in0=t_raw[:], scalar1=FMAX, scalar2=C_INF, op0=ALU.is_le, op1=ALU.add),
                lambda: nc.vector.tensor_scalar(out=t_down[:], in0=t_raw[:], scalar1=-FMAX, scalar2=C_INF, op0=ALU.is_ge, op1=ALU.add),
                lambda: nc.vector.tensor_scalar(out=t_raw[:], in0=t_raw[:], scalar1=-FMAX, scalar2=FMAX, op0=ALU.max, op1=ALU.min),
                lambda: nc.vector.tensor_tensor(out=t_up[:], in0=t_up[:], in1=t_down[:], op=ALU.mult),
                lambda: nc.vector.tensor_tensor(out=t_coord[:], in0=t_raw[:], in1=t_up[:], op=ALU.mult),
            ]

        def spread_times(g):
            bank = turn_pool.tile([P, BANK], F32, name="t_turned", tag="turn")
            t_turned[g] = bank
            for ii in range(GROUP):
                i = GROUP * g + ii
                nc.tensor.transpose(
                    out=bank[:, ii * P : (ii + 1) * P],
                    in_=t_coord[:, i : i + 1].to_broadcast([P, P]),
                    identity=ident[:],
                )

        def copy_times(g):
            g0 = g - MIDDLE // 2
            nc.vector.tensor_copy(out=t_row[:, g0 * BANK : (g0 + 1) * BANK], in_=t_turned[g][:])

        def temperature():
            return [
                lambda: nc.vector.tensor_scalar(out=tau[:], in0=scale_raw[:], scalar1=0.01, scalar2=2.5, op0=ALU.max, op1=ALU.min),
                lambda: nc.vector.tensor_tensor(out=is_number[:], in0=scale_raw[:], in1=scale_raw[:], op=ALU.is_equal),
                lambda: nc.vector.scalar_tensor_tensor(
                    out=minus_4tau[:], in0=tau[:], scalar=-4.0, in1=is_number[:], op0=ALU.mult, op1=ALU.mult
                ),
            ]

        h_codes = [keep.tile([P, GROUP * P], U32, name="h_codes%d" % g, align_bytes=64) for g in range(GROUPS)]
        h_scales = [keep.tile([P, GROUP * P], U8, name="h_scales%d" % g, align_bytes=64) for g in range(GROUPS)]
        factor_up_tile = a_pool.tile([P, 4 * BANK], F32, name="factor_up_tile", tag="a")
        factor_down_tile = a_pool.tile([P, 4 * BANK], F32, name="factor_down_tile", tag="a")
        factor_up = factor_up_tile[:].bitcast(BF16)
        factor_down = factor_down_tile[:].bitcast(BF16)
        grouped_of = {}
        turned_of = {}

        def sanitise(g0, g1):
            n = (g1 - g0) * GROUP
            first = (g0 % 2) * GROUP
            x = h_raw[g0 // 2][:].rearrange("p (i c) -> p i c", c=SLOT)[:, first : first + n, 2 : K + 2]
            c0 = first * K if n == GROUP else 0
            up, down = factor_up[:, c0 : c0 + n * K], factor_down[:, c0 : c0 + n * K]
            up3 = up.rearrange("p (i c) -> p i c", c=K)
            down3 = down.rearrange("p (i c) -> p i c", c=K)
            return [
                lambda: nc.vector.tensor_scalar(out=up3, in0=x, scalar1=FMAX, scalar2=C_INF, op0=ALU.is_le, op1=ALU.add),
                lambda: nc.vector.tensor_scalar(out=down3, in0=x, scalar1=-FMAX, scalar2=C_INF, op0=ALU.is_ge, op1=ALU.add),
                lambda: nc.vector.tensor_scalar(out=x, in0=x, scalar1=-FMAX, scalar2=FMAX, op0=ALU.max, op1=ALU.min),
                lambda: nc.vector.tensor_tensor(out=up, in0=up, in1=down, op=ALU.mult),
                lambda: nc.vector.tensor_tensor(out=x, in0=x, in1=up3, op=ALU.mult),
            ]

        def h_transpose(g):
            for pair in range(2):
                turned = turn_pool.tile([P, BANK], F32, name="turned", tag="turn")
                turned_of[(g, pair)] = turned
                for ii in range(2):
                    i = GROUP * g + 2 * pair + ii
                    words = h_raw[i // CHUNK][:].bitcast(F32)
                    base = (i % CHUNK) * (SLOT // 2) + 1
                    for u in range(2):
                        nc.tensor.transpose(
                            out=turned[:, u * 2 * P + ii * P : u * 2 * P + (ii + 1) * P],
                            in_=words[:, base + u * P : base + (u + 1) * P],
                            identity=ident[:],
                        )

        def h_copy_out(g):
            copy = nc.vector.tensor_copy if g >= 6 else nc.scalar.copy
            grouped_of[g] = grouped_pool.tile([P, GROUP * K], BF16, name="grouped", tag="grouped", align_bytes=64)
            words = grouped_of[g][:].bitcast(F32).rearrange("p (t u) -> p t u", u=2)
            for pair in range(2):
                copy(
                    out=words[:, pair * 2 * P : (pair + 1) * 2 * P, :],
                    in_=turned_of[(g, pair)][:].rearrange("p (u t) -> p t u", u=2),
                )

        def h_quantise(g):
            nc.vector.quantize_mx(out=h_codes[g][:].bitcast(FP8X4), scales=h_scales[g][:], in_=grouped_of[g][:])

        sumsq = keep.tile([P, W_TILES], F32, name="sumsq")
        squares = keep.tile([P, K], BF16, name="squares")
        row_ok = keep.tile([P, W_TILES], F32, name="row_ok")
        sum_cut = keep.tile([P, W_TILES], F32, name="sum_cut")
        halves = keep.tile([P, W_TILES], F32, name="halves")
        squares_v = keep.tile([P, K], F32, name="squares_v")
        nc.gpsimd.memset(halves[:], 0.5)
        norm = keep.tile([P, W_TILES], F32, name="norm")
        e_plus = keep.tile([P, W_TILES], F32, name="e_plus")
        e_minus = keep.tile([P, W_TILES], F32, name="e_minus")
        inverse = keep.tile([P, W_TILES], F32, name="inverse")
        diff = keep.tile([P, W_TILES], F32, name="diff")
        total = keep.tile([P, W_TILES], F32, name="total")
        r_col = keep.tile([P, W_TILES], F32, name="r_col")
        cosh_col = keep.tile([P, W_TILES], F32, name="cosh_col")

        def w_row_tile(j):
            return w_raw[j // 2][:, (j % 2) * K : (j % 2 + 1) * K]

        cosh_row = keep.tile([P, VOCAB], F32, name="cosh_row")
        spread_of = {}

        def spread(h):
            bank = sum_pool.tile([P, BANK], F32, name="spread", tag="sum")
            spread_of[h] = bank
            for jj in range(4):
                j = 4 * h + jj
                nc.tensor.transpose(
                    out=bank[:, jj * P : (jj + 1) * P],
                    in_=cosh_col[:, j : j + 1].to_broadcast([P, P]),
                    identity=ident[:],
                )

        def spread_copy(h):
            nc.scalar.copy(out=cosh_row[:, h * BANK : (h + 1) * BANK], in_=spread_of[h][:])

        w_space_tile = x_pool.tile([P, 4 * BANK], F32, name="w_space_tile", tag="x", align_bytes=64)
        w_space = w_space_tile[:].bitcast(BF16)
        w_grouped_tile = x_pool.tile([P, 4 * BANK], F32, name="w_grouped_tile", tag="x", align_bytes=64)
        w_grouped = [w_grouped_tile[:, h * 2 * BANK : (h + 1) * 2 * BANK].bitcast(BF16) for h in range(2)]
        w_codes = keep.tile([P, VOCAB], U32, name="w_codes", align_bytes=64)
        w_scales = keep.tile([P, VOCAB], U8, name="w_scales", align_bytes=64)
        w_turned = {}

        def w_scale(j):
            nc.scalar.activation(
                out=w_space[:, j * K : (j + 1) * K].rearrange("p (u e q) -> p u e q", u=2, e=2),
                in_=w_row_tile(j).rearrange("p (u q e) -> p u e q", u=2, e=2),
                func=ACT.Copy,
                scale=r_col[:, j : j + 1],
            )

        def w_transpose(q):
            turned = turn_pool.tile([P, 2 * BANK], BF16, name="w_turned", tag="turn")
            w_turned[q] = turned
            for jj in range(2):
                for t in range(4):
                    nc.tensor.transpose(
                        out=turned[:, (jj * 4 + t) * P : (jj * 4 + t + 1) * P],
                        in_=w_space[:, (2 * q + jj) * K + t * P : (2 * q + jj) * K + (t + 1) * P],
                        identity=ident_bf[:],
                    )

        def w_copy_out(copy, q):
            copy(
                out=w_grouped[q // 2][:, (q % 2) * 2 * BANK : (q % 2 + 1) * 2 * BANK].rearrange(
                    "p (j v t) -> p j v t", j=2, t=4
                ),
                in_=w_turned[q][:].rearrange("p (j t v) -> p j v t", j=2, t=4),
            )

        def w_quantise(h):
            nc.vector.quantize_mx(
                out=w_codes[:, h * BANK : (h + 1) * BANK].bitcast(FP8X4),
                scales=w_scales[:, h * BANK : (h + 1) * BANK],
                in_=w_grouped[h],
            )

        dot_of = {}
        x_of = {}
        a_of = {}

        def dot(u):
            for k in range(4):
                bank = sum_pool.tile([P, BANK], F32, name="dot", tag="sum")
                dot_of[(u, k)] = bank
                if u >= MIDDLE:
                    g, j = u // 2, 4 * (u % 2) + k
                    nc.tensor.matmul_mx(
                        out=bank[:],
                        lhsT=w_codes[:, j * P : (j + 1) * P].bitcast(FP8X4),
                        lhsT_scale=w_scales[:, j * P : (j + 1) * P],
                        rhs=h_codes[g][:].bitcast(FP8X4),
                        rhs_scale=h_scales[g][:],
                        start=True,
                        stop=True,
                    )
                    continue
                i, h = 2 * u + k // 2, k % 2
                g = i // GROUP
                tokens = slice((i % GROUP) * P, (i % GROUP + 1) * P)
                nc.tensor.matmul_mx(
                    out=bank[:],
                    lhsT=h_codes[g][:, tokens].bitcast(FP8X4),
                    lhsT_scale=h_scales[g][:, tokens],
                    rhs=w_codes[:, h * BANK : (h + 1) * BANK].bitcast(FP8X4),
                    rhs_scale=w_scales[:, h * BANK : (h + 1) * BANK],
                    start=True,
                    stop=True,
                )

        def make_x(u):
            x_of[u] = x_pool.tile([P, 4 * BANK], F32, name="x", tag="x", align_bytes=64)
            x4 = x_of[u][:].rearrange("p (i j c) -> p j i c", i=4, j=4)
            for k in range(4):
                if u >= MIDDLE:
                    g, j = u // 2 - MIDDLE // 2, 4 * (u % 2) + k
                    nc.vector.scalar_tensor_tensor(
                        out=x4[:, k, :, :],
                        in0=t_row[:, g * BANK : (g + 1) * BANK].rearrange("p (i c) -> p i c", i=4),
                        scalar=cosh_col[:, j : j + 1],
                        in1=dot_of[(u, k)][:].rearrange("p (i c) -> p i c", i=4),
                        op0=ALU.mult,
                        op1=ALU.subtract,
                    )
                    continue
                i, h = 2 * u + k // 2, k % 2
                nc.vector.scalar_tensor_tensor(
                    out=x_of[u][:, k * BANK : (k + 1) * BANK],
                    in0=cosh_row[:, h * BANK : (h + 1) * BANK],
                    scalar=t_coord[:, i : i + 1],
                    in1=dot_of[(u, k)][:],
                    op0=ALU.mult,
                    op1=ALU.subtract,
                )

        def gated_clip(u):
            gate = gate_pool.tile([P, 1], F32, name="gate", tag="gate")
            nc.vector.memset(gate[:], X_MIN)
            x = x_of[u][:]
            nc.gpsimd.tensor_scalar(out=x, in0=x, scalar1=X_MAX, scalar2=gate[:, 0:1], op0=ALU.min, op1=ALU.max)

        def clip(eng, u, c0=0, c1=4 * BANK):
            x = x_of[u][:, c0:c1]
            eng.tensor_scalar(out=x, in0=x, scalar1=X_MAX, scalar2=X_MIN, op0=ALU.min, op1=ALU.max)

        def roots(u):
            a_of[u] = a_pool.tile([P, 4 * BANK], F32, name="a", tag="a")
            if u in SCALAR_CLIPS:
                nc.scalar.activation(out=x_of[u][:], in_=x_of[u][:], func=ACT.Relu, bias=minus_one[:, 0:1])
                nc.scalar.activation(out=a_of[u][:], in_=x_of[u][:], func=ACT.Sqrt, bias=one[:, 0:1], scale=0.5)
                nc.scalar.activation(out=x_of[u][:], in_=x_of[u][:], func=ACT.Sqrt, bias=floor_b[:, 0:1], scale=0.5)
                return
            nc.scalar.activation(out=a_of[u][:], in_=x_of[u][:], func=ACT.Sqrt, bias=half[:, 0:1], scale=0.5)
            nc.scalar.activation(out=x_of[u][:], in_=x_of[u][:], func=ACT.Sqrt, bias=minus_half[:, 0:1], scale=0.5)

        def add_roots(u):
            nc.vector.tensor_tensor(out=a_of[u][:], in0=a_of[u][:], in1=x_of[u][:], op=ALU.add)

        def square(u):
            nc.scalar.activation(out=a_of[u][:], in_=a_of[u][:], func=ACT.Square)
            nc.vector.tensor_scalar(out=a_of[u][:], in0=a_of[u][:], scalar1=minus_4tau[:, 0:1], scalar2=None, op0=ALU.mult)
            nc.sync.dma_start(out=out_flat[:, 4 * BANK * u : 4 * BANK * (u + 1)], in_=a_of[u][:])

        sum_of = {}

        def sum_on_tensor(u, k):
            c = slice(k * BANK, (k + 1) * BANK)
            bank = turn_pool.tile([P, BANK], F32, name="root_sum", tag="turn")
            sum_of[(u, k)] = bank
            nc.tensor.matmul(out=bank[:], lhsT=ident[:], rhs=a_of[u][:, c], start=True, stop=False)
            nc.tensor.matmul(out=bank[:], lhsT=ident[:], rhs=x_of[u][:, c], start=False, stop=True)

        def logarithm_of_sum(u, k):
            c = slice(k * BANK, (k + 1) * BANK)
            nc.scalar.activation(out=a_of[u][:, c], in_=sum_of[(u, k)][:], func=ACT.Ln)

        def turn_and_add(u, ii):
            bank = turn_pool.tile([P, BANK], F32, name="root_sum", tag="turn")
            sum_of[(u, ii)] = bank
            for jj in range(4):
                c = slice((4 * ii + jj) * P, (4 * ii + jj + 1) * P)
                for part in (a_of[u], x_of[u]):
                    nc.tensor.matmul(
                        out=bank[:, jj * P : (jj + 1) * P],
                        lhsT=part[:, c],
                        rhs=ident[:],
                        start=part is a_of[u],
                        stop=part is x_of[u],
                        is_transpose=True,
                    )

        def finish_turned(u, i0, i1):
            a = a_of[u][:, i0 * BANK : i1 * BANK]
            nc.vector.scalar_tensor_tensor(out=a, in0=a, scalar=minus_4tau[:, 0:1], in1=a, op0=ALU.mult, op1=ALU.mult)
            g, h = u // 2, u % 2
            nc.sync.dma_start(
                out=out_tiles[:, GROUP * g + i0 : GROUP * g + i1, h * BANK : (h + 1) * BANK],
                in_=a.rearrange("p (i v) -> p i v", v=BANK),
            )

        def logarithm(u, c0=0, c1=4 * BANK):
            nc.scalar.activation(out=a_of[u][:, c0:c1], in_=a_of[u][:, c0:c1], func=ACT.Ln)

        def finish(u, c0=0, c1=4 * BANK):
            a = a_of[u][:, c0:c1]
            nc.vector.scalar_tensor_tensor(out=a, in0=a, scalar=minus_4tau[:, 0:1], in1=a, op0=ALU.mult, op1=ALU.mult)
            nc.sync.dma_start(out=out_flat[:, 4 * BANK * u + c0 : 4 * BANK * u + c1], in_=a)

        for j in range(W_TILES):
            nc.scalar.activation(out=squares[:], in_=w_row_tile(j), func=ACT.Square, accum_out=sumsq[:, j : j + 1])
        first_half = sanitise(0, 1)
        second_half = sanitise(1, 2)
        for step in first_half[:4] + second_half[:1] + first_half[4:] + second_half[1:2]:
            step()
        h_transpose(0)
        nc.vector.tensor_scalar(out=sum_cut[:], in0=sumsq[:], scalar1=1.0e-30, scalar2=SUMSQ_MAX, op0=ALU.max, op1=ALU.min)
        nc.gpsimd.tensor_tensor(out=norm[:], in0=sum_cut[:], in1=halves[:], op=ALU.pow)
        nc.scalar.activation(out=e_plus[:], in_=norm[:], func=ACT.Exp)
        nc.scalar.activation(out=e_minus[:], in_=norm[:], func=ACT.Exp, scale=-1.0)
        nc.vector.tensor_single_scalar(out=row_ok[:], in_=sumsq[:], scalar=FMAX, op=ALU.is_le)
        nc.vector.tensor_scalar(out=w_all, in0=w_all, scalar1=-FMAX, scalar2=FMAX, op0=ALU.max, op1=ALU.min)
        nc.vector.reciprocal(out=inverse[:], in_=norm[:])
        nc.vector.tensor_tensor(out=diff[:], in0=e_plus[:], in1=e_minus[:], op=ALU.subtract)
        nc.vector.tensor_tensor(out=total[:], in0=e_plus[:], in1=e_minus[:], op=ALU.add)
        nc.vector.scalar_tensor_tensor(out=diff[:], in0=diff[:], scalar=0.5, in1=inverse[:], op0=ALU.mult, op1=ALU.mult)
        nc.vector.scalar_tensor_tensor(out=cosh_col[:], in0=total[:], scalar=0.5, in1=row_ok[:], op0=ALU.mult, op1=ALU.mult)
        nc.vector.scalar_tensor_tensor(out=r_col[:], in0=diff[:], scalar=1.0, in1=row_ok[:], op0=ALU.max, op1=ALU.mult)
        ahead = sanitise(2, 4)
        for step in second_half[2:4] + ahead[:1] + second_half[4:]:
            step()
        for h in range(2):
            for j in range(4 * h, 4 * h + 4):
                w_scale(j)
            w_transpose(2 * h)
            w_transpose(2 * h + 1)
            spread(h)
            if h == 0:
                h_copy_out(0)
                for step, short in zip(ahead[1:4], temperature()):
                    step()
                    short()
                h_quantise(0)
            w_copy_out(nc.scalar.copy, 2 * h)
            w_copy_out(nc.scalar.copy, 2 * h + 1)
            spread_copy(h)
            if h == 0:
                gather_times()
                times = time_coordinates()
                times[0]()
                times[1]()
                w_quantise(0)
                times[2]()
                times[3]()
                times[4]()
            else:
                w_quantise(1)
        h_transpose(1)
        h_copy_out(1)
        nc.scalar.activation(out=scratch[:], in_=one[:], func=ACT.Sqrt)
        late = [(ahead[4], 4)]
        for c in range(2, TILES // CHUNK):
            late.extend(zip(sanitise(2 * c, 2 * c + 2), (2 * c, 2 * c, 2 * c, 2 * c, 2 * c + 2)))
        ready = 2
        turned = 2
        quantised = 1

        first = 0
        previous = []
        dot(0)
        for size in BATCHES:
            batch = list(range(first, first + size))
            first += size
            early = [(u, k) for u in batch if u in EARLY_SUMS for k in range(4)]
            late_sums = [(u, k) for u in batch if u in LATE_SUMS for k in range(4)]
            summed = []
            for k, u in enumerate(batch):
                make_x(u)
                steps = []
                if quantised < turned and 2 * quantised <= u + 3:
                    steps.append(partial(h_quantise, quantised))
                    quantised += 1
                turning = turned < ready and (turned < 6 or u >= 8)
                if turning:
                    h_transpose(turned)
                if u + 1 < UNITS:
                    dot(u + 1)
                if previous:
                    steps.append(partial(finish, previous.pop(0)))
                for n in range(2 if u % 3 == 1 else 1):
                    if late:
                        step, ready = late.pop(0)
                        steps.append(step)
                if u in VECTOR_CLIPS:
                    steps.append(partial(clip, nc.vector, u))
                if 8 <= u < 8 + GROUPS - MIDDLE // 2:
                    spread_times(MIDDLE // 2 + u - 8)
                if 8 < u <= 8 + GROUPS - MIDDLE // 2:
                    steps.insert(0, partial(copy_times, MIDDLE // 2 + u - 1 - 8))
                for step in steps[:-1]:
                    step()
                if u not in SCALAR_CLIPS + VECTOR_CLIPS:
                    gated_clip(u)
                if steps:
                    steps[-1]()
                if early and k > early[0][0] - batch[0] + 3 and turned >= 6:
                    summed.append(early.pop(0))
                    sum_on_tensor(*summed[-1])
                if turning:
                    h_copy_out(turned)
                    turned += 1
                if k > 0 and u - 1 not in SCALAR_CLIPS:
                    roots(u - 1)
                if u in SCALAR_CLIPS:
                    roots(u)
            while early:
                summed.append(early.pop(0))
                sum_on_tensor(*summed[-1])
            if batch[-1] not in SCALAR_CLIPS:
                roots(batch[-1])
            for u in previous:
                finish(u)
            pieces = ((0, 4 * BANK),) if first < UNITS else ((0, 2 * BANK), (2 * BANK, 4 * BANK))
            others = [u for u in batch if u not in EARLY_SUMS + LATE_SUMS and u < MIDDLE]
            turned_units = [u for u in batch if u >= MIDDLE]
            for s in summed:
                logarithm_of_sum(*s)
            for s in late_sums:
                sum_on_tensor(*s)
            for u in others:
                add_roots(u)
            tail = []
            for n in range(max(len(others), len(turned_units))):
                tail.extend(others[n : n + 1] + turned_units[n : n + 1])
            for u in tail:
                if u < MIDDLE:
                    for c0, c1 in pieces:
                        logarithm(u, c0, c1)
                else:
                    for ii in range(4):
                        turn_and_add(u, ii)
                        logarithm_of_sum(u, ii)
            for s in late_sums:
                logarithm_of_sum(*s)
            previous = [u for u in batch if u in EARLY_SUMS] + tail + [u for u in batch if u in LATE_SUMS]
        for u in previous:
            if u >= MIDDLE:
                n = 1 if u == UNITS - 1 else 2
                for ii in range(0, 4, n):
                    finish_turned(u, ii, ii + n)
            elif u in EARLY_SUMS + LATE_SUMS:
                for k in range(4):
                    finish(u, k * BANK, (k + 1) * BANK)
            else:
                for c0, c1 in pieces:
                    finish(u, c0, c1)
